import numpy as np
import ml_dtypes


def mxq(x, axis, fmt="e4m3"):
    dtype, down = {"e4m3": (ml_dtypes.float8_e4m3fn, 7), "e5m2": (ml_dtypes.float8_e5m2, 14)}[fmt]
    v = np.moveaxis(np.asarray(x, np.float32).astype(ml_dtypes.bfloat16).astype(np.float64), axis, -1)
    blocks = v.reshape(v.shape[:-1] + (-1, 32))
    amax = np.abs(blocks).max(-1, keepdims=True)
    byte = np.maximum(np.where(amax > 0, np.frexp(amax)[1] - 1 + 127, 0) - down, 1)
    scale = np.exp2(byte - 127.0)
    codes = (blocks / scale).astype(np.float32).astype(dtype).astype(np.float64)
    return np.moveaxis((codes * scale).reshape(v.shape), -1, axis)


WIDE = False


def mx_kscale(k):
    if not WIDE:
        return np.ones(k)
    levels = np.array([10, -10, 5, -5, 0])
    if k % 512:
        return np.exp2(np.random.permutation(np.resize(levels, k // 32))).repeat(32)
    a = np.empty((k // 512, 16))
    for p in range(k // 512):
        a[p, :8] = np.random.permutation(np.resize(levels, 8))
        for g in range(8):
            far = levels[np.abs(levels - a[p, g]) >= 10]
            a[p, g + 8] = far[np.random.randint(len(far))]
    return np.exp2(a.ravel()).repeat(32)


BF16 = ml_dtypes.bfloat16


def bf(x):
    return np.asarray(x, np.float32).astype(BF16)


def f64(x):
    return np.asarray(x).astype(np.float64)


B, D, A = 1024, 1024, 1024


def setup_inputs():
    s = mx_kscale(D)
    return {
        "x": bf(np.random.standard_normal((B, D)) * s),
        "saved_x": bf(np.random.standard_normal((B, D)) * s),
        "saved_a": bf(np.random.standard_normal((B, A))),
        "saved_b": bf(0.5 + np.random.random((B, A))),
        "saved_p": bf(np.random.standard_normal((B, A))),
        "time_decay": bf(np.random.standard_normal(A)),
        "time_first": bf(np.random.standard_normal(A)),
        "k_mixed": bf(np.random.random(D)),
        "v_mixed": bf(np.random.random(D)),
        "key_weight": bf(np.random.standard_normal((D, A)) / np.sqrt(D) / s[:, None]),
        "value_weight": bf(np.random.standard_normal((D, A)) / np.sqrt(D) / s[:, None]),
    }


def reference(x, saved_x, saved_a, saved_b, saved_p, time_decay, time_first, k_mixed, v_mixed, key_weight, value_weight):
    x, saved_x = f64(x), f64(saved_x)
    saved_a, saved_b, saved_p = f64(saved_a), f64(saved_b), f64(saved_p)
    time_decay, time_first = f64(time_decay), f64(time_first)
    k_mixed, v_mixed = f64(k_mixed), f64(v_mixed)
    xk = x * k_mixed + saved_x * (1.0 - k_mixed)
    xv = x * v_mixed + saved_x * (1.0 - v_mixed)
    k = mxq(xk, 1, "e4m3") @ mxq(f64(key_weight), 0, "e4m3")
    v = mxq(xv, 1, "e4m3") @ mxq(f64(value_weight), 0, "e4m3")
    w = k + time_first
    p = np.maximum(saved_p, w)
    e1 = np.exp(saved_p - p)
    e2 = np.exp(w - p)
    wkv = (e1 * saved_a + e2 * v) / (e1 * saved_b + e2)
    w2 = saved_p + time_decay
    p2 = np.maximum(w2, k)
    f1 = np.exp(w2 - p2)
    f2 = np.exp(k - p2)
    aa = f1 * saved_a + f2 * v
    bb = f1 * saved_b + f2
    return wkv, aa, bb, p2

@@ -1,0 +1,374 @@
+from contextlib import ExitStack
+
+import concourse.mybir as mybir
+from concourse.masks import make_identity
+
+F32 = mybir.dt.float32
+BF16 = mybir.dt.bfloat16
+U32 = mybir.dt.uint32
+U8 = mybir.dt.uint8
+FP8X4 = mybir.dt.float8_e4m3fn_x4
+ALU = mybir.AluOpType
+FUNC = mybir.ActivationFunctionType
+
+P = 128
+PACK = 4
+K_PASS = P * PACK
+ROWS = 1024
+DEPTH = 1024
+WIDTH = 1024
+PASSES = DEPTH // K_PASS
+CHUNKS = DEPTH // P
+ROW_TILES = ROWS // P
+N_TILE = 512
+ROW_HALVES = ROWS // N_TILE
+BLOCKS = N_TILE // P
+COL_BLOCKS = WIDTH // P
+TILES = ROW_HALVES * COL_BLOCKS
+FACTOR_BANKS = ("e1_ps", "e2_ps", "f1_ps", "f2_ps")
+GROUP = 4
+VECTOR_SHARE = 640
+assert BLOCKS == GROUP
+
+FLOPS = 2 * 2 * ROWS * DEPTH * WIDTH
+
+
+def interleave(nc, grouped, planes):
+    nc.vector.tensor_copy(
+        out=grouped[:, 0:VECTOR_SHARE, :].rearrange("p (c i) t -> p c t i", i=4),
+        in_=planes[:, :, 0:VECTOR_SHARE].rearrange("p t (c i) -> p c t i", i=4),
+    )
+    nc.scalar.copy(
+        out=grouped[:, VECTOR_SHARE:, :].rearrange("p (c i) t -> p c t i", i=4),
+        in_=planes[:, :, VECTOR_SHARE:].rearrange("p t (c i) -> p c t i", i=4),
+    )
+
+
+def quantise(nc, grouped, codes, scales):
+    nc.vector.quantize_mx(
+        out=codes.bitcast(FP8X4),
+        scales=scales,
+        in_=grouped.rearrange("p c t -> p (c t)"),
+    )
+
+
+def tile_rwkv_attention_pa_kernel(
+    tc,
+    x,
+    saved_x,
+    saved_a,
+    saved_b,
+    saved_p,
+    time_decay,
+    time_first,
+    k_mixed,
+    v_mixed,
+    key_weight,
+    value_weight,
+    out_0,
+    out_1,
+    out_2,
+    out_3,
+):
+    nc = tc.nc
+    with ExitStack() as pools:
+        pools.enter_context(tc.manual_schedule())
+        keep = pools.enter_context(tc.tile_pool(name="keep", bufs=1))
+        early = pools.enter_context(tc.psum_pool(name="early", bufs=1))
+
+        xk_codes = keep.tile([P, PASSES, ROWS], U32, align_bytes=64)
+        xv_codes = keep.tile([P, PASSES, ROWS], U32, align_bytes=64)
+        wk_codes = keep.tile([P, PASSES, WIDTH], U32, align_bytes=64)
+        wv_codes = keep.tile([P, PASSES, WIDTH], U32, align_bytes=64)
+        xk_scales = keep.tile([P, PASSES, ROWS], U8, align_bytes=64)
+        xv_scales = keep.tile([P, PASSES, ROWS], U8, align_bytes=64)
+        wk_scales = keep.tile([P, PASSES, WIDTH], U8, align_bytes=64)
+        wv_scales = keep.tile([P, PASSES, WIDTH], U8, align_bytes=64)
+        p_rows = keep.tile([P, ROW_TILES, WIDTH], BF16)
+        decay_rows = keep.tile([P, WIDTH], BF16)
+        ident = keep.tile([P, P], BF16)
+        ident_f32 = keep.tile([P, P], F32)
+        vector_rows = keep.tile([P, K_PASS], BF16)
+        columns = keep.tile([P, 4 * CHUNKS], F32)
+        one_minus_mix = keep.tile([P, 2 * CHUNKS], F32)
+        shift = keep.tile([P, CHUNKS], F32)
+        minus_shift = keep.tile([P, CHUNKS], F32)
+        mix = columns[:, 0 : 2 * CHUNKS]
+        decay = columns[:, 2 * CHUNKS : 3 * CHUNKS]
+        first = columns[:, 3 * CHUNKS : 4 * CHUNKS]
+
+        with ExitStack() as operand_pools:
+            whole = operand_pools.enter_context(tc.tile_pool(name="whole", bufs=1))
+            stage = operand_pools.enter_context(tc.tile_pool(name="stage", bufs=2))
+            group = operand_pools.enter_context(tc.tile_pool(name="group", bufs=4))
+            turned = operand_pools.enter_context(tc.psum_pool(name="turned", bufs=2))
+
+            nc.vector.memset(vector_rows[:], 0.0)
+            for n, vector in enumerate((k_mixed, v_mixed, time_decay, time_first)):
+                nc.sync.dma_start(
+                    out=vector_rows[n * PASSES : (n + 1) * PASSES, :],
+                    in_=vector.rearrange("(g k) -> g k", k=K_PASS),
+                )
+            x_rows = whole.tile([P, ROW_TILES, DEPTH], BF16)
+            s_rows = whole.tile([P, ROW_TILES, DEPTH], BF16)
+            wk_planes = whole.tile([P, PASSES, PACK, WIDTH], BF16)
+            wv_planes = whole.tile([P, PASSES, PACK, WIDTH], BF16)
+            x_view = x.rearrange("(r p) d -> p r d", p=P)
+            s_view = saved_x.rearrange("(r p) d -> p r d", p=P)
+            wk_view = key_weight.rearrange("(g p t) a -> g p t a", t=PACK, p=P)
+            wv_view = value_weight.rearrange("(g p t) a -> g p t a", t=PACK, p=P)
+            nc.sync.dma_start(out=wk_planes[:, 0], in_=wk_view[0])
+            nc.sync.dma_start(out=wv_planes[:, 0], in_=wv_view[0])
+            for g in range(PASSES):
+                depth = slice(g * K_PASS, (g + 1) * K_PASS)
+                nc.sync.dma_start(out=s_rows[:, :, depth], in_=s_view[:, :, depth])
+                nc.sync.dma_start(out=x_rows[:, :, depth], in_=x_view[:, :, depth])
+            nc.sync.dma_start(out=wk_planes[:, 1], in_=wk_view[1])
+            nc.sync.dma_start(out=wv_planes[:, 1], in_=wv_view[1])
+            nc.sync.dma_start(out=decay_rows[:], in_=time_decay.partition_broadcast(P))
+            nc.sync.dma_start(out=p_rows[:], in_=saved_p.rearrange("(r p) a -> p r a", p=P))
+
+            make_identity(nc, ident[:])
+            make_identity(nc, ident_f32[:])
+            mix_turned = turned.tile([P, PACK, P], BF16, tag="x_turned")
+            shift_turned = turned.tile([P, PACK, P], BF16, tag="s_turned")
+            for t in range(PACK):
+                nc.tensor.transpose(mix_turned[:, t, :], vector_rows[:, t:K_PASS:PACK], ident[:])
+                nc.tensor.transpose(
+                    shift_turned[:, t, :], vector_rows[:, t * P : (t + 1) * P], ident[:]
+                )
+            for source, half in ((mix_turned, 0), (shift_turned, 1)):
+                nc.vector.tensor_copy(
+                    out=columns[:, half * 2 * CHUNKS : (half + 1) * 2 * CHUNKS].rearrange(
+                        "p (r t) -> p r t", t=PACK
+                    ),
+                    in_=source[:, :, half * 2 * PASSES : (half + 1) * 2 * PASSES].rearrange(
+                        "p t r -> p r t"
+                    ),
+                )
+            nc.vector.tensor_scalar(
+                out=one_minus_mix[:], in0=mix, scalar1=-1.0, scalar2=1.0, op0=ALU.mult, op1=ALU.add
+            )
+            nc.vector.tensor_tensor(out=shift[:], in0=decay, in1=first, op=ALU.add)
+            nc.vector.tensor_scalar_mul(out=minus_shift[:], in0=shift[:], scalar1=-1.0)
+
+            s_words = s_rows[:].bitcast(F32)
+            x_words = x_rows[:].bitcast(F32)
+
+            def quantise_pair(g, k_source, v_source, k_codes, k_scales, v_codes, v_scales):
+                k_grouped = group.tile([P, WIDTH, PACK], BF16, tag="grouped", align_bytes=64)
+                v_grouped = group.tile([P, WIDTH, PACK], BF16, tag="grouped", align_bytes=64)
+                interleave(nc, k_grouped[:], k_source)
+                interleave(nc, v_grouped[:], v_source)
+                quantise(nc, k_grouped[:], k_codes[:, g, :], k_scales[:, g, :])
+                quantise(nc, v_grouped[:], v_codes[:, g, :], v_scales[:, g, :])
+
+            def mix_pass(g):
+                k_planes = stage.tile([P, PACK, ROWS], BF16)
+                v_planes = stage.tile([P, PACK, ROWS], BF16)
+                for u in range(PACK // 2):
+                    picked = slice(g * K_PASS // 2 + u, (g + 1) * K_PASS // 2, 2)
+                    for h in range(ROW_HALVES):
+                        s_turned = turned.tile([P, N_TILE], F32)
+                        x_turned = turned.tile([P, N_TILE], F32)
+                        for bank, words in ((s_turned, s_words), (x_turned, x_words)):
+                            for b in range(BLOCKS):
+                                nc.tensor.transpose(
+                                    bank[:, b * P : (b + 1) * P],
+                                    words[:, h * BLOCKS + b, picked],
+                                    ident_f32[:],
+                                )
+                        s_pairs = s_turned[:].bitcast(BF16)
+                        x_pairs = x_turned[:].bitcast(BF16)
+                        for e in range(2):
+                            t = 2 * u + e
+                            c = g * PACK + t
+                            for planes, col in ((k_planes, c), (v_planes, CHUNKS + c)):
+                                old_part = stage.tile([P, N_TILE], F32, bufs=4)
+                                nc.scalar.activation(
+                                    out=old_part[:],
+                                    in_=s_pairs[:, e::2],
+                                    func=FUNC.Copy,
+                                    scale=one_minus_mix[:, col : col + 1],
+                                )
+                                nc.vector.scalar_tensor_tensor(
+                                    out=planes[:, t, h * N_TILE : (h + 1) * N_TILE],
+                                    in0=x_pairs[:, e::2],
+                                    scalar=mix[:, col : col + 1],
+                                    in1=old_part[:],
+                                    op0=ALU.mult,
+                                    op1=ALU.add,
+                                )
+                return k_planes, v_planes
+
+            for g in range(PASSES):
+                quantise_pair(
+                    g, wk_planes[:, g], wv_planes[:, g], wk_codes, wk_scales, wv_codes, wv_scales
+                )
+                k_planes, v_planes = mix_pass(g)
+                quantise_pair(g, k_planes[:], v_planes[:], xk_codes, xk_scales, xv_codes, xv_scales)
+
+        late = pools.enter_context(tc.tile_pool(name="late", bufs=1, reuse_waits="tile"))
+        work = pools.enter_context(tc.tile_pool(name="work", bufs=2, reuse_waits="tile"))
+        banks = pools.enter_context(tc.psum_pool(name="banks", bufs=1, reuse_waits="tile"))
+        a_rows = late.tile([P, ROW_TILES, WIDTH], BF16)
+        b_rows = late.tile([P, ROW_TILES, WIDTH], BF16)
+        for h in range(ROW_HALVES):
+            blocks = slice(h * BLOCKS, (h + 1) * BLOCKS)
+            for rows_tile, source in ((a_rows, saved_a), (b_rows, saved_b)):
+                nc.sync.dma_start(
+                    out=rows_tile[:, blocks, :],
+                    in_=source.rearrange("(r p) a -> p r a", p=P)[:, blocks, :],
+                )
+
+        def rows_of(i, b=0, count=BLOCKS):
+            first_row = (i // COL_BLOCKS) * N_TILE + b * P
+            return slice(first_row, first_row + count * P)
+
+        def blocks_of(i):
+            return slice((i // COL_BLOCKS) * BLOCKS, (i // COL_BLOCKS + 1) * BLOCKS)
+
+        def cols_of(i, count=1):
+            return slice((i % COL_BLOCKS) * P, (i % COL_BLOCKS + count) * P)
+
+        def project(i):
+            k_ps = early.tile([P, BLOCKS, P], F32)
+            v_ps = early.tile([P, BLOCKS, P], F32)
+            for acc, x_codes, x_scales, w_codes, w_scales in (
+                (k_ps, xk_codes, xk_scales, wk_codes, wk_scales),
+                (v_ps, xv_codes, xv_scales, wv_codes, wv_scales),
+            ):
+                for b in range(BLOCKS):
+                    for g in range(PASSES):
+                        nc.tensor.matmul_mx(
+                            out=acc[:, b, :],
+                            lhsT=x_codes[:, g, rows_of(i, b, 1)].bitcast(FP8X4),
+                            lhsT_scale=x_scales[:, g, rows_of(i, b, 1)],
+                            rhs=w_codes[:, g, cols_of(i)].bitcast(FP8X4),
+                            rhs_scale=w_scales[:, g, cols_of(i)],
+                            start=(g == 0),
+                            stop=(g == PASSES - 1),
+                        )
+            v_rows = work.tile([P, BLOCKS, P], F32, bufs=4)
+            nc.scalar.copy(out=v_rows[:], in_=v_ps[:])
+            decayed = work.tile([P, BLOCKS, P], F32, bufs=3)
+            nc.gpsimd.tensor_tensor(
+                out=decayed[:],
+                in0=p_rows[:, blocks_of(i), cols_of(i)],
+                in1=decay_rows[:, cols_of(i)].unsqueeze(1).to_broadcast([P, BLOCKS, P]),
+                op=ALU.add,
+            )
+            return k_ps, v_rows, decayed
+
+        def compare(i, k_ps, decayed, p2):
+            j = i % COL_BLOCKS
+            lead = work.tile([P, BLOCKS, P], F32)
+            nc.vector.tensor_tensor(out=lead[:], in0=k_ps[:], in1=decayed[:], op=ALU.subtract)
+            nc.vector.tensor_tensor(out=p2, in0=k_ps[:], in1=decayed[:], op=ALU.max)
+            lead_turned = early.tile([P, N_TILE], F32)
+            for b in range(BLOCKS):
+                nc.tensor.transpose(lead_turned[:, b * P : (b + 1) * P], lead[:, b, :], ident_f32[:])
+            e1_raw = work.tile([P, N_TILE], F32)
+            e2_raw = work.tile([P, N_TILE], F32)
+            f1_raw = work.tile([P, N_TILE], F32)
+            f2_raw = work.tile([P, N_TILE], F32)
+            nc.scalar.activation(
+                out=e1_raw[:], in_=lead_turned[:], func=FUNC.Exp, scale=-1.0, bias=minus_shift[:, j : j + 1]
+            )
+            nc.scalar.activation(
+                out=e2_raw[:], in_=lead_turned[:], func=FUNC.Exp, bias=shift[:, j : j + 1]
+            )
+            nc.scalar.activation(out=f1_raw[:], in_=lead_turned[:], func=FUNC.Exp, scale=-1.0)
+            nc.scalar.activation(out=f2_raw[:], in_=lead_turned[:], func=FUNC.Exp)
+            return e1_raw, e2_raw, f1_raw, f2_raw
+
+        def upright(turned_tile, name):
+            bank = banks.tile([P, BLOCKS, P], F32, name=name)
+            for b in range(BLOCKS):
+                nc.tensor.transpose(bank[:, b, :], turned_tile[:, b * P : (b + 1) * P], ident_f32[:])
+            return bank
+
+        def clamped(out, raw, other, op):
+            nc.vector.scalar_tensor_tensor(
+                out=out, in0=raw[:], scalar=1.0, in1=other, op0=ALU.min, op1=op
+            )
+
+        def blend(i, factor_banks, v_rows, aa, bb, num, den):
+            e1_ps, e2_ps, f1_ps, f2_ps = factor_banks
+            a_part = a_rows[:, blocks_of(i), cols_of(i)]
+            b_part = b_rows[:, blocks_of(i), cols_of(i)]
+            e2_v = work.tile([P, BLOCKS, P], F32)
+            f2_v = work.tile([P, BLOCKS, P], F32)
+            clamped(num, e1_ps, a_part, ALU.mult)
+            clamped(den, e1_ps, b_part, ALU.mult)
+            clamped(e2_v[:], e2_ps, v_rows[:], ALU.mult)
+            clamped(den, e2_ps, den, ALU.add)
+            nc.gpsimd.tensor_tensor(out=num, in0=num, in1=e2_v[:], op=ALU.add)
+            clamped(aa, f1_ps, a_part, ALU.mult)
+            clamped(bb, f1_ps, b_part, ALU.mult)
+            clamped(f2_v[:], f2_ps, v_rows[:], ALU.mult)
+            clamped(bb, f2_ps, bb, ALU.add)
+            nc.gpsimd.tensor_tensor(out=aa, in0=aa, in1=f2_v[:], op=ALU.add)
+
+        def store(out, group_tile, q):
+            first_tile = q * GROUP
+            nc.sync.dma_start(
+                out=out.rearrange("(r p) a -> p r a", p=P)[
+                    :, blocks_of(first_tile), cols_of(first_tile, GROUP)
+                ],
+                in_=group_tile[:].rearrange("p b n c -> p b (n c)"),
+            )
+
+        upright_in = {0: project(0)}
+        raw = {}
+        factor_in = {}
+        grouped_out = {}
+        for s in range(-2, TILES + GROUP):
+            if s + 2 < TILES:
+                i = s + 2
+                if i % GROUP == 0:
+                    p2_group = work.tile([P, BLOCKS, GROUP, P], F32)
+                raw[i] = compare(i, upright_in[i][0], upright_in[i][2], p2_group[:, :, i % GROUP, :])
+                if i % GROUP == GROUP - 1:
+                    store(out_3, p2_group, i // GROUP)
+            if s + 3 < TILES:
+                upright_in[s + 3] = project(s + 3)
+            if 0 <= s < TILES:
+                n = s % GROUP
+                if n == 0:
+                    aa_group = work.tile([P, BLOCKS, GROUP, P], F32)
+                    bb_group = work.tile([P, BLOCKS, GROUP, P], F32)
+                    num_group = work.tile([P, BLOCKS, GROUP, P], F32)
+                    den_group = work.tile([P, BLOCKS, GROUP, P], F32)
+                    grouped_out[s // GROUP] = (num_group, den_group)
+                blend(
+                    s,
+                    factor_in[s],
+                    upright_in[s][1],
+                    aa_group[:, :, n, :],
+                    bb_group[:, :, n, :],
+                    num_group[:, :, n, :],
+                    den_group[:, :, n, :],
+                )
+                if n == GROUP - 1:
+                    store(out_1, aa_group, s // GROUP)
+                    store(out_2, bb_group, s // GROUP)
+            if 0 <= s + 1 < TILES:
+                factor_in[s + 1] = [
+                    upright(raw[s + 1][n], name) for n, name in enumerate(FACTOR_BANKS)
+                ]
+            if s >= GROUP:
+                q = s // GROUP - 1
+                b = s % GROUP
+                num_done, den_done = grouped_out[q]
+                if b == 0:
+                    nc.scalar.activation(out=den_done[:], in_=den_done[:], func=FUNC.Ln)
+                nc.scalar.activation(out=den_done[:, b], in_=den_done[:, b], func=FUNC.Exp, scale=-1.0)
+                wkv_rows = work.tile([P, GROUP, P], F32, bufs=3)
+                nc.gpsimd.tensor_tensor(
+                    out=wkv_rows[:], in0=num_done[:, b], in1=den_done[:, b], op=ALU.mult
+                )
+                nc.sync.dma_start(
+                    out=out_0[rows_of(q * GROUP, b, 1), cols_of(q * GROUP, GROUP)],
+                    in_=wkv_rows[:].rearrange("p n c -> p (n c)"),
+                )

@@ -25,9 +25,10 @@ ROW_HALVES = ROWS // N_TILE
 BLOCKS = N_TILE // P
 COL_BLOCKS = WIDTH // P
 TILES = ROW_HALVES * COL_BLOCKS
-FACTOR_BANKS = ("e1_ps", "e2_ps", "f1_ps", "f2_ps")
+FACTOR_BANKS = ("e_ps", "f1_ps", "f2_ps")
 GROUP = 4
 VECTOR_SHARE = 640
+E_CAP = 2.0**60
 assert BLOCKS == GROUP
 
 FLOPS = 2 * 2 * ROWS * DEPTH * WIDTH
@@ -92,7 +93,6 @@ def tile_rwkv_attention_pa_kernel(
         columns = keep.tile([P, 4 * CHUNKS], F32)
         one_minus_mix = keep.tile([P, 2 * CHUNKS], F32)
         shift = keep.tile([P, CHUNKS], F32)
-        minus_shift = keep.tile([P, CHUNKS], F32)
         mix = columns[:, 0 : 2 * CHUNKS]
         decay = columns[:, 2 * CHUNKS : 3 * CHUNKS]
         first = columns[:, 3 * CHUNKS : 4 * CHUNKS]
@@ -150,7 +150,6 @@ def tile_rwkv_attention_pa_kernel(
                 out=one_minus_mix[:], in0=mix, scalar1=-1.0, scalar2=1.0, op0=ALU.mult, op1=ALU.add
             )
             nc.vector.tensor_tensor(out=shift[:], in0=decay, in1=first, op=ALU.add)
-            nc.vector.tensor_scalar_mul(out=minus_shift[:], in0=shift[:], scalar1=-1.0)
 
             s_words = s_rows[:].bitcast(F32)
             x_words = x_rows[:].bitcast(F32)
@@ -268,19 +267,15 @@ def tile_rwkv_attention_pa_kernel(
             lead_turned = early.tile([P, N_TILE], F32)
             for b in range(BLOCKS):
                 nc.tensor.transpose(lead_turned[:, b * P : (b + 1) * P], lead[:, b, :], ident_f32[:])
-            e1_raw = work.tile([P, N_TILE], F32)
-            e2_raw = work.tile([P, N_TILE], F32)
+            e_raw = work.tile([P, N_TILE], F32)
             f1_raw = work.tile([P, N_TILE], F32)
             f2_raw = work.tile([P, N_TILE], F32)
             nc.scalar.activation(
-                out=e1_raw[:], in_=lead_turned[:], func=FUNC.Exp, scale=-1.0, bias=minus_shift[:, j : j + 1]
-            )
-            nc.scalar.activation(
-                out=e2_raw[:], in_=lead_turned[:], func=FUNC.Exp, bias=shift[:, j : j + 1]
+                out=e_raw[:], in_=lead_turned[:], func=FUNC.Exp, bias=shift[:, j : j + 1]
             )
             nc.scalar.activation(out=f1_raw[:], in_=lead_turned[:], func=FUNC.Exp, scale=-1.0)
             nc.scalar.activation(out=f2_raw[:], in_=lead_turned[:], func=FUNC.Exp)
-            return e1_raw, e2_raw, f1_raw, f2_raw
+            return e_raw, f1_raw, f2_raw
 
         def upright(turned_tile, name):
             bank = banks.tile([P, BLOCKS, P], F32, name=name)
@@ -288,22 +283,20 @@ def tile_rwkv_attention_pa_kernel(
                 nc.tensor.transpose(bank[:, b, :], turned_tile[:, b * P : (b + 1) * P], ident_f32[:])
             return bank
 
-        def clamped(out, raw, other, op):
+        def clamped(out, raw, other, op, cap=1.0):
             nc.vector.scalar_tensor_tensor(
-                out=out, in0=raw[:], scalar=1.0, in1=other, op0=ALU.min, op1=op
+                out=out, in0=raw[:], scalar=cap, in1=other, op0=ALU.min, op1=op
             )
 
         def blend(i, factor_banks, v_rows, aa, bb, num, den):
-            e1_ps, e2_ps, f1_ps, f2_ps = factor_banks
+            e_ps, f1_ps, f2_ps = factor_banks
             a_part = a_rows[:, blocks_of(i), cols_of(i)]
             b_part = b_rows[:, blocks_of(i), cols_of(i)]
-            e2_v = work.tile([P, BLOCKS, P], F32)
+            e_v = work.tile([P, BLOCKS, P], F32)
             f2_v = work.tile([P, BLOCKS, P], F32)
-            clamped(num, e1_ps, a_part, ALU.mult)
-            clamped(den, e1_ps, b_part, ALU.mult)
-            clamped(e2_v[:], e2_ps, v_rows[:], ALU.mult)
-            clamped(den, e2_ps, den, ALU.add)
-            nc.gpsimd.tensor_tensor(out=num, in0=num, in1=e2_v[:], op=ALU.add)
+            clamped(e_v[:], e_ps, v_rows[:], ALU.mult, E_CAP)
+            clamped(den, e_ps, b_part, ALU.add, E_CAP)
+            nc.gpsimd.tensor_tensor(out=num, in0=e_v[:], in1=a_part, op=ALU.add)
             clamped(aa, f1_ps, a_part, ALU.mult)
             clamped(bb, f1_ps, b_part, ALU.mult)
             clamped(f2_v[:], f2_ps, v_rows[:], ALU.mult)

@@ -19,30 +19,52 @@ DEPTH = 1024
 WIDTH = 1024
 PASSES = DEPTH // K_PASS
 CHUNKS = DEPTH // P
-ROW_TILES = ROWS // P
 N_TILE = 512
 ROW_HALVES = ROWS // N_TILE
+COL_HALVES = WIDTH // N_TILE
 BLOCKS = N_TILE // P
 COL_BLOCKS = WIDTH // P
 TILES = ROW_HALVES * COL_BLOCKS
 FACTOR_BANKS = ("e_ps", "f1_ps", "f2_ps")
 GROUP = 4
-VECTOR_SHARE = 640
+PAIR = 2
+CHUNK = PACK * N_TILE * 2
+AT_HIDDEN_1 = 0
+AT_WEIGHTS_1 = 4 * CHUNK
+AT_PLANES = 8 * CHUNK
+AT_GROUPED = 12 * CHUNK
+AT_OLD = 16 * CHUNK
+AT_HIDDEN_0 = 18 * CHUNK
+AT_WEIGHTS_0 = 22 * CHUNK
+AT_P2 = AT_HIDDEN_0
+AT_AA = AT_HIDDEN_0 + 2 * CHUNK
+AT_BB = AT_WEIGHTS_0
+AT_P1 = AT_WEIGHTS_0 + 2 * CHUNK
+AT_QUOTIENT = 26 * CHUNK
 E_CAP = 2.0**60
-assert BLOCKS == GROUP
+AHEAD = 2
+SUM_AHEAD = 7
 
 FLOPS = 2 * 2 * ROWS * DEPTH * WIDTH
 
 
-def interleave(nc, grouped, planes):
-    nc.vector.tensor_copy(
-        out=grouped[:, 0:VECTOR_SHARE, :].rearrange("p (c i) t -> p c t i", i=4),
-        in_=planes[:, :, 0:VECTOR_SHARE].rearrange("p t (c i) -> p c t i", i=4),
-    )
-    nc.scalar.copy(
-        out=grouped[:, VECTOR_SHARE:, :].rearrange("p (c i) t -> p c t i", i=4),
-        in_=planes[:, :, VECTOR_SHARE:].rearrange("p t (c i) -> p c t i", i=4),
-    )
+def interleave(nc, grouped, planes, shares):
+    first = 0
+    for engine, count in zip("vsg", shares):
+        cols = slice(first, first + count)
+        first += count
+        if count == 0:
+            continue
+        out = grouped[:, cols, :].rearrange("p (c i) t -> p c t i", i=4)
+        in_ = planes[:, :, cols].rearrange("p t (c i) -> p c t i", i=4)
+        if engine == "v":
+            nc.vector.tensor_copy(out=out, in_=in_)
+        elif engine == "s":
+            nc.scalar.copy(out=out, in_=in_)
+        else:
+            nc.gpsimd.tensor_scalar(
+                out=out, in0=in_, scalar1=1.0, scalar2=0.0, op0=ALU.mult, op1=ALU.add
+            )
 
 
 def quantise(nc, grouped, codes, scales):
@@ -75,6 +97,8 @@ def tile_rwkv_attention_pa_kernel(
     with ExitStack() as pools:
         pools.enter_context(tc.manual_schedule())
         keep = pools.enter_context(tc.tile_pool(name="keep", bufs=1))
+        arena = pools.enter_context(tc.tile_pool(name="arena", bufs=1))
+        work = pools.enter_context(tc.tile_pool(name="work", bufs=2))
         early = pools.enter_context(tc.psum_pool(name="early", bufs=1))
 
         xk_codes = keep.tile([P, PASSES, ROWS], U32, align_bytes=64)
@@ -85,7 +109,6 @@ def tile_rwkv_attention_pa_kernel(
         xv_scales = keep.tile([P, PASSES, ROWS], U8, align_bytes=64)
         wk_scales = keep.tile([P, PASSES, WIDTH], U8, align_bytes=64)
         wv_scales = keep.tile([P, PASSES, WIDTH], U8, align_bytes=64)
-        p_rows = keep.tile([P, ROW_TILES, WIDTH], BF16)
         decay_rows = keep.tile([P, WIDTH], BF16)
         ident = keep.tile([P, P], BF16)
         ident_f32 = keep.tile([P, P], F32)
@@ -96,12 +119,102 @@ def tile_rwkv_attention_pa_kernel(
         mix = columns[:, 0 : 2 * CHUNKS]
         decay = columns[:, 2 * CHUNKS : 3 * CHUNKS]
         first = columns[:, 3 * CHUNKS : 4 * CHUNKS]
+        p0_rows = keep.tile([P, BLOCKS, WIDTH], BF16)
+        a0_rows = keep.tile([P, BLOCKS, WIDTH], BF16)
+        b0_rows = keep.tile([P, BLOCKS, WIDTH], BF16)
 
-        with ExitStack() as operand_pools:
-            whole = operand_pools.enter_context(tc.tile_pool(name="whole", bufs=1))
-            stage = operand_pools.enter_context(tc.tile_pool(name="stage", bufs=2))
-            group = operand_pools.enter_context(tc.tile_pool(name="group", bufs=4))
-            turned = operand_pools.enter_context(tc.psum_pool(name="turned", bufs=2))
+        def half_of(source, h):
+            return source.rearrange("(h r p) d -> h p r d", r=BLOCKS, p=P)[h]
+
+        def turn_pair(pool, g, u, x_rows, s_rows):
+            picked = slice(u, K_PASS // 2, 2)
+            s_turned = pool.tile([P, N_TILE], F32, name="s_turned")
+            x_turned = pool.tile([P, N_TILE], F32, name="x_turned")
+            for bank, rows in ((s_turned, s_rows), (x_turned, x_rows)):
+                words = rows[:].bitcast(F32)
+                for b in range(BLOCKS):
+                    nc.tensor.transpose(
+                        bank[:, b * P : (b + 1) * P], words[:, b, picked], ident_f32[:]
+                    )
+            return s_turned, x_turned
+
+        def scale_pair(g, u, s_turned):
+            s_pairs = s_turned[:].bitcast(BF16)
+            old_parts = []
+            for e in range(2):
+                c = g * PACK + 2 * u + e
+                for col in (c, CHUNKS + c):
+                    old_part = arena.tile([P, N_TILE], F32, bufs=4, offset=AT_OLD)
+                    nc.scalar.activation(
+                        out=old_part[:],
+                        in_=s_pairs[:, e::2],
+                        func=FUNC.Copy,
+                        scale=one_minus_mix[:, col : col + 1],
+                    )
+                    old_parts.append(old_part)
+            return old_parts
+
+        def add_pair(g, u, x_turned, old_parts, k_planes, v_planes):
+            x_pairs = x_turned[:].bitcast(BF16)
+            for e in range(2):
+                t = 2 * u + e
+                c = g * PACK + t
+                for n, (planes, col) in enumerate(((k_planes, c), (v_planes, CHUNKS + c))):
+                    nc.vector.scalar_tensor_tensor(
+                        out=planes[:, t, :],
+                        in0=x_pairs[:, e::2],
+                        scalar=mix[:, col : col + 1],
+                        in1=old_parts[2 * e + n][:],
+                        op0=ALU.mult,
+                        op1=ALU.add,
+                    )
+
+        codes_of = {"xk": xk_codes, "xv": xv_codes, "wk": wk_codes, "wv": wv_codes}
+        scales_of = {"xk": xk_scales, "xv": xv_scales, "wk": wk_scales, "wv": wv_scales}
+        planes_of = {}
+        grouped_of = {}
+        pair_of = {}
+        hidden_of = {}
+
+        def load_hidden(h, g):
+            depth = slice(g * K_PASS, (g + 1) * K_PASS)
+            at = (AT_HIDDEN_0, AT_HIDDEN_1)[h] + 2 * g * CHUNK
+            s_rows = arena.tile([P, BLOCKS, K_PASS], BF16, name=f"s{h}{g}", offset=at)
+            x_rows = arena.tile([P, BLOCKS, K_PASS], BF16, name=f"x{h}{g}", offset=at + CHUNK)
+            nc.sync.dma_start(out=s_rows[:], in_=half_of(saved_x, h)[:, :, depth])
+            nc.sync.dma_start(out=x_rows[:], in_=half_of(x, h)[:, :, depth])
+            hidden_of[h, g] = (x_rows, s_rows)
+
+        def turn(pool, h, g, u):
+            pair_of[h, g, u] = turn_pair(pool, g, u, *hidden_of[h, g])
+
+        def scale(h, g, u):
+            s_turned, x_turned = pair_of[h, g, u]
+            pair_of[h, g, u] = (x_turned, scale_pair(g, u, s_turned))
+
+        def add(h, g, u):
+            if u == 0:
+                for name in ("xk", "xv"):
+                    planes = arena.tile([P, PACK, N_TILE], BF16, bufs=4, offset=AT_PLANES)
+                    planes_of[name, h, g] = planes[:]
+            add_pair(g, u, *pair_of[h, g, u], planes_of["xk", h, g], planes_of["xv", h, g])
+
+        def regroup(name, h, g, shares):
+            grouped = arena.tile(
+                [P, N_TILE, PACK], BF16, bufs=4, align_bytes=64, offset=AT_GROUPED
+            )
+            interleave(nc, grouped[:], planes_of[name, h, g], shares)
+            grouped_of[name, h, g] = grouped
+
+        def pack(name, h, g):
+            part = slice(h * N_TILE, (h + 1) * N_TILE)
+            quantise(
+                nc, grouped_of[name, h, g][:], codes_of[name][:, g, part], scales_of[name][:, g, part]
+            )
+
+        turned = pools.enter_context(tc.psum_pool(name="turned", bufs=1))
+        with ExitStack() as first_pools:
+            turned_first = first_pools.enter_context(tc.psum_pool(name="turned_first", bufs=1))
 
             nc.vector.memset(vector_rows[:], 0.0)
             for n, vector in enumerate((k_mixed, v_mixed, time_decay, time_first)):
@@ -109,24 +222,32 @@ def tile_rwkv_attention_pa_kernel(
                     out=vector_rows[n * PASSES : (n + 1) * PASSES, :],
                     in_=vector.rearrange("(g k) -> g k", k=K_PASS),
                 )
-            x_rows = whole.tile([P, ROW_TILES, DEPTH], BF16)
-            s_rows = whole.tile([P, ROW_TILES, DEPTH], BF16)
-            wk_planes = whole.tile([P, PASSES, PACK, WIDTH], BF16)
-            wv_planes = whole.tile([P, PASSES, PACK, WIDTH], BF16)
-            x_view = x.rearrange("(r p) d -> p r d", p=P)
-            s_view = saved_x.rearrange("(r p) d -> p r d", p=P)
-            wk_view = key_weight.rearrange("(g p t) a -> g p t a", t=PACK, p=P)
-            wv_view = value_weight.rearrange("(g p t) a -> g p t a", t=PACK, p=P)
-            nc.sync.dma_start(out=wk_planes[:, 0], in_=wk_view[0])
-            nc.sync.dma_start(out=wv_planes[:, 0], in_=wv_view[0])
+            w_views = {
+                "wk": key_weight.rearrange("(g p t) a -> g p t a", t=PACK, p=P),
+                "wv": value_weight.rearrange("(g p t) a -> g p t a", t=PACK, p=P),
+            }
+            w_planes = {}
+
+            def load_weights(c, g):
+                for name in ("wk", "wv"):
+                    at = (AT_WEIGHTS_0, AT_WEIGHTS_1)[c] + (2 * g + (name == "wv")) * CHUNK
+                    planes = arena.tile([P, PACK, N_TILE], BF16, name=f"{name}{c}{g}", offset=at)
+                    nc.sync.dma_start(
+                        out=planes[:], in_=w_views[name][g][:, :, c * N_TILE : (c + 1) * N_TILE]
+                    )
+                    planes_of[name, c, g] = planes[:]
+
             for g in range(PASSES):
-                depth = slice(g * K_PASS, (g + 1) * K_PASS)
-                nc.sync.dma_start(out=s_rows[:, :, depth], in_=s_view[:, :, depth])
-                nc.sync.dma_start(out=x_rows[:, :, depth], in_=x_view[:, :, depth])
-            nc.sync.dma_start(out=wk_planes[:, 1], in_=wk_view[1])
-            nc.sync.dma_start(out=wv_planes[:, 1], in_=wv_view[1])
+                load_hidden(0, g)
+                load_weights(0, g)
             nc.sync.dma_start(out=decay_rows[:], in_=time_decay.partition_broadcast(P))
-            nc.sync.dma_start(out=p_rows[:], in_=saved_p.rearrange("(r p) a -> p r a", p=P))
+            nc.sync.dma_start(out=p0_rows[:], in_=half_of(saved_p, 0))
+            load_hidden(1, 0)
+            for g in range(PASSES):
+                load_weights(1, g)
+            load_hidden(1, 1)
+            nc.sync.dma_start(out=a0_rows[:], in_=half_of(saved_a, 0))
+            nc.sync.dma_start(out=b0_rows[:], in_=half_of(saved_b, 0))
 
             make_identity(nc, ident[:])
             make_identity(nc, ident_f32[:])
@@ -151,74 +272,53 @@ def tile_rwkv_attention_pa_kernel(
             )
             nc.vector.tensor_tensor(out=shift[:], in0=decay, in1=first, op=ALU.add)
 
-            s_words = s_rows[:].bitcast(F32)
-            x_words = x_rows[:].bitcast(F32)
+            V, S, G = (512, 0, 0), (0, 512, 0), (0, 0, 512)
+            regroup("wk", 0, 0, G)
+            regroup("wv", 0, 0, G)
+            turn(turned, 0, 0, 0)
+            turn(turned_first, 0, 0, 1)
+            scale(0, 0, 0)
+            add(0, 0, 0)
+            turn(turned, 0, 1, 0)
+            scale(0, 0, 1)
+            add(0, 0, 1)
+            turn(turned_first, 0, 1, 1)
+            scale(0, 1, 0)
+            add(0, 1, 0)
+            regroup("xk", 0, 0, S)
+            pack("wk", 0, 0)
+            pack("wv", 0, 0)
+            regroup("wk", 0, 1, G)
+            regroup("wv", 0, 1, G)
+            scale(0, 1, 1)
+            add(0, 1, 1)
+            pack("xk", 0, 0)
+            regroup("xv", 0, 0, S)
+            regroup("xk", 0, 1, V)
+            pack("wk", 0, 1)
+            regroup("xv", 0, 1, V)
+            pack("xk", 0, 1)
+            pack("wv", 0, 1)
+            turn(turned, 1, 0, 0)
+            pack("xv", 0, 0)
+            pack("xv", 0, 1)
+            regroup("wk", 1, 0, S)
+            scale(1, 0, 0)
 
-            def quantise_pair(g, k_source, v_source, k_codes, k_scales, v_codes, v_scales):
-                k_grouped = group.tile([P, WIDTH, PACK], BF16, tag="grouped", align_bytes=64)
-                v_grouped = group.tile([P, WIDTH, PACK], BF16, tag="grouped", align_bytes=64)
-                interleave(nc, k_grouped[:], k_source)
-                interleave(nc, v_grouped[:], v_source)
-                quantise(nc, k_grouped[:], k_codes[:, g, :], k_scales[:, g, :])
-                quantise(nc, v_grouped[:], v_codes[:, g, :], v_scales[:, g, :])
-
-            def mix_pass(g):
-                k_planes = stage.tile([P, PACK, ROWS], BF16)
-                v_planes = stage.tile([P, PACK, ROWS], BF16)
-                for u in range(PACK // 2):
-                    picked = slice(g * K_PASS // 2 + u, (g + 1) * K_PASS // 2, 2)
-                    for h in range(ROW_HALVES):
-                        s_turned = turned.tile([P, N_TILE], F32)
-                        x_turned = turned.tile([P, N_TILE], F32)
-                        for bank, words in ((s_turned, s_words), (x_turned, x_words)):
-                            for b in range(BLOCKS):
-                                nc.tensor.transpose(
-                                    bank[:, b * P : (b + 1) * P],
-                                    words[:, h * BLOCKS + b, picked],
-                                    ident_f32[:],
-                                )
-                        s_pairs = s_turned[:].bitcast(BF16)
-                        x_pairs = x_turned[:].bitcast(BF16)
-                        for e in range(2):
-                            t = 2 * u + e
-                            c = g * PACK + t
-                            for planes, col in ((k_planes, c), (v_planes, CHUNKS + c)):
-                                old_part = stage.tile([P, N_TILE], F32, bufs=4)
-                                nc.scalar.activation(
-                                    out=old_part[:],
-                                    in_=s_pairs[:, e::2],
-                                    func=FUNC.Copy,
-                                    scale=one_minus_mix[:, col : col + 1],
-                                )
-                                nc.vector.scalar_tensor_tensor(
-                                    out=planes[:, t, h * N_TILE : (h + 1) * N_TILE],
-                                    in0=x_pairs[:, e::2],
-                                    scalar=mix[:, col : col + 1],
-                                    in1=old_part[:],
-                                    op0=ALU.mult,
-                                    op1=ALU.add,
-                                )
-                return k_planes, v_planes
-
-            for g in range(PASSES):
-                quantise_pair(
-                    g, wk_planes[:, g], wv_planes[:, g], wk_codes, wk_scales, wv_codes, wv_scales
-                )
-                k_planes, v_planes = mix_pass(g)
-                quantise_pair(g, k_planes[:], v_planes[:], xk_codes, xk_scales, xv_codes, xv_scales)
-
-        late = pools.enter_context(tc.tile_pool(name="late", bufs=1, reuse_waits="tile"))
-        work = pools.enter_context(tc.tile_pool(name="work", bufs=2, reuse_waits="tile"))
         banks = pools.enter_context(tc.psum_pool(name="banks", bufs=1, reuse_waits="tile"))
-        a_rows = late.tile([P, ROW_TILES, WIDTH], BF16)
-        b_rows = late.tile([P, ROW_TILES, WIDTH], BF16)
-        for h in range(ROW_HALVES):
-            blocks = slice(h * BLOCKS, (h + 1) * BLOCKS)
-            for rows_tile, source in ((a_rows, saved_a), (b_rows, saved_b)):
-                nc.sync.dma_start(
-                    out=rows_tile[:, blocks, :],
-                    in_=source.rearrange("(r p) a -> p r a", p=P)[:, blocks, :],
-                )
+        p1_rows = arena.tile([P, BLOCKS, WIDTH], BF16, offset=AT_P1)
+        nc.sync.dma_start(out=p1_rows[:], in_=half_of(saved_p, 1))
+        p_halves = [p0_rows, p1_rows]
+        a_halves = [a0_rows]
+        b_halves = [b0_rows]
+
+        def load_second_state():
+            a1_rows = arena.tile([P, BLOCKS, WIDTH], BF16, offset=AT_HIDDEN_1)
+            b1_rows = arena.tile([P, BLOCKS, WIDTH], BF16, offset=AT_HIDDEN_1 + 2 * CHUNK)
+            nc.sync.dma_start(out=a1_rows[:], in_=half_of(saved_a, 1))
+            nc.sync.dma_start(out=b1_rows[:], in_=half_of(saved_b, 1))
+            a_halves.append(a1_rows)
+            b_halves.append(b1_rows)
 
         def rows_of(i, b=0, count=BLOCKS):
             first_row = (i // COL_BLOCKS) * N_TILE + b * P
@@ -230,34 +330,43 @@ def tile_rwkv_attention_pa_kernel(
         def cols_of(i, count=1):
             return slice((i % COL_BLOCKS) * P, (i % COL_BLOCKS + count) * P)
 
-        def project(i):
+        def part_of(halves, i):
+            return halves[i // COL_BLOCKS][:, :, cols_of(i)]
+
+        def project(i, acc, x_codes, x_scales, w_codes, w_scales):
+            for b in range(BLOCKS):
+                for g in range(PASSES):
+                    nc.tensor.matmul_mx(
+                        out=acc[:, b, :],
+                        lhsT=x_codes[:, g, rows_of(i, b, 1)].bitcast(FP8X4),
+                        lhsT_scale=x_scales[:, g, rows_of(i, b, 1)],
+                        rhs=w_codes[:, g, cols_of(i)].bitcast(FP8X4),
+                        rhs_scale=w_scales[:, g, cols_of(i)],
+                        start=(g == 0),
+                        stop=(g == PASSES - 1),
+                    )
+
+        def project_k(i):
             k_ps = early.tile([P, BLOCKS, P], F32)
-            v_ps = early.tile([P, BLOCKS, P], F32)
-            for acc, x_codes, x_scales, w_codes, w_scales in (
-                (k_ps, xk_codes, xk_scales, wk_codes, wk_scales),
-                (v_ps, xv_codes, xv_scales, wv_codes, wv_scales),
-            ):
-                for b in range(BLOCKS):
-                    for g in range(PASSES):
-                        nc.tensor.matmul_mx(
-                            out=acc[:, b, :],
-                            lhsT=x_codes[:, g, rows_of(i, b, 1)].bitcast(FP8X4),
-                            lhsT_scale=x_scales[:, g, rows_of(i, b, 1)],
-                            rhs=w_codes[:, g, cols_of(i)].bitcast(FP8X4),
-                            rhs_scale=w_scales[:, g, cols_of(i)],
-                            start=(g == 0),
-                            stop=(g == PASSES - 1),
-                        )
-            v_rows = work.tile([P, BLOCKS, P], F32, bufs=4)
-            nc.scalar.copy(out=v_rows[:], in_=v_ps[:])
-            decayed = work.tile([P, BLOCKS, P], F32, bufs=3)
+            project(i, k_ps, xk_codes, xk_scales, wk_codes, wk_scales)
+            return k_ps
+
+        def decay_state(i):
+            decayed = work.tile([P, BLOCKS, P], F32, bufs=SUM_AHEAD + 1)
             nc.gpsimd.tensor_tensor(
                 out=decayed[:],
-                in0=p_rows[:, blocks_of(i), cols_of(i)],
+                in0=part_of(p_halves, i),
                 in1=decay_rows[:, cols_of(i)].unsqueeze(1).to_broadcast([P, BLOCKS, P]),
                 op=ALU.add,
             )
-            return k_ps, v_rows, decayed
+            return decayed
+
+        def project_v(i):
+            v_ps = early.tile([P, BLOCKS, P], F32)
+            project(i, v_ps, xv_codes, xv_scales, wv_codes, wv_scales)
+            v_rows = work.tile([P, BLOCKS, P], F32, bufs=3)
+            nc.scalar.copy(out=v_rows[:], in_=v_ps[:])
+            return v_rows
 
         def compare(i, k_ps, decayed, p2):
             j = i % COL_BLOCKS
@@ -267,9 +376,9 @@ def tile_rwkv_attention_pa_kernel(
             lead_turned = early.tile([P, N_TILE], F32)
             for b in range(BLOCKS):
                 nc.tensor.transpose(lead_turned[:, b * P : (b + 1) * P], lead[:, b, :], ident_f32[:])
-            e_raw = work.tile([P, N_TILE], F32)
-            f1_raw = work.tile([P, N_TILE], F32)
-            f2_raw = work.tile([P, N_TILE], F32)
+            e_raw = work.tile([P, N_TILE], F32, bufs=AHEAD)
+            f1_raw = work.tile([P, N_TILE], F32, bufs=AHEAD)
+            f2_raw = work.tile([P, N_TILE], F32, bufs=AHEAD)
             nc.scalar.activation(
                 out=e_raw[:], in_=lead_turned[:], func=FUNC.Exp, bias=shift[:, j : j + 1]
             )
@@ -288,80 +397,143 @@ def tile_rwkv_attention_pa_kernel(
                 out=out, in0=raw[:], scalar=cap, in1=other, op0=ALU.min, op1=op
             )
 
-        def blend(i, factor_banks, v_rows, aa, bb, num, den):
+        def blend(i, factor_banks, v_rows, aa, bb, num, den, adder):
             e_ps, f1_ps, f2_ps = factor_banks
-            a_part = a_rows[:, blocks_of(i), cols_of(i)]
-            b_part = b_rows[:, blocks_of(i), cols_of(i)]
-            e_v = work.tile([P, BLOCKS, P], F32)
+            a_part = part_of(a_halves, i)
+            b_part = part_of(b_halves, i)
+            f1_a = work.tile([P, BLOCKS, P], F32)
             f2_v = work.tile([P, BLOCKS, P], F32)
-            clamped(e_v[:], e_ps, v_rows[:], ALU.mult, E_CAP)
+            clamped(num, e_ps, v_rows[:], ALU.mult, E_CAP)
             clamped(den, e_ps, b_part, ALU.add, E_CAP)
-            nc.gpsimd.tensor_tensor(out=num, in0=e_v[:], in1=a_part, op=ALU.add)
-            clamped(aa, f1_ps, a_part, ALU.mult)
+            nc.gpsimd.tensor_tensor(out=num, in0=num, in1=a_part, op=ALU.add)
+            clamped(f1_a[:], f1_ps, a_part, ALU.mult)
             clamped(bb, f1_ps, b_part, ALU.mult)
             clamped(f2_v[:], f2_ps, v_rows[:], ALU.mult)
             clamped(bb, f2_ps, bb, ALU.add)
-            nc.gpsimd.tensor_tensor(out=aa, in0=aa, in1=f2_v[:], op=ALU.add)
+            adder.tensor_tensor(out=aa, in0=f1_a[:], in1=f2_v[:], op=ALU.add)
 
-        def store(out, group_tile, q):
-            first_tile = q * GROUP
+        def store(out, pair_tile, i):
             nc.sync.dma_start(
-                out=out.rearrange("(r p) a -> p r a", p=P)[
-                    :, blocks_of(first_tile), cols_of(first_tile, GROUP)
-                ],
-                in_=group_tile[:].rearrange("p b n c -> p b (n c)"),
+                out=out.rearrange("(r p) a -> p r a", p=P)[:, blocks_of(i), cols_of(i, PAIR)],
+                in_=pair_tile[:].rearrange("p b n c -> p b (n c)"),
             )
 
-        upright_in = {0: project(0)}
+        early_jobs = {
+
+            0: [(scale, 1, 0, 1)],
+            1: [(scale, 1, 1, 0)],
+            2: [(scale, 1, 1, 1)],
+        }
+        late_jobs = {
+
+            -2: [(regroup, "wv", 1, 0, V), (pack, "wk", 1, 0)],
+            -1: [(add, 1, 0, 0), (pack, "wv", 1, 0), (turn, turned, 1, 0, 1), (regroup, "wk", 1, 1, S)],
+            0: [(regroup, "wv", 1, 1, V), (pack, "wk", 1, 1), (add, 1, 0, 1), (pack, "wv", 1, 1), (turn, turned, 1, 1, 0), (regroup, "xk", 1, 0, S)],
+            1: [(add, 1, 1, 0), (pack, "xk", 1, 0), (turn, turned, 1, 1, 1), (regroup, "xv", 1, 0, S)],
+            2: [(load_second_state,), (add, 1, 1, 1), (pack, "xv", 1, 0), (regroup, "xk", 1, 1, S)],
+            3: [(pack, "xk", 1, 1), (regroup, "xv", 1, 1, S)],
+            4: [(pack, "xv", 1, 1)],
+        }
+
+        k_in = {0: project_k(0)}
+        v_in = {}
+        decayed_in = {i: decay_state(i) for i in range(SUM_AHEAD)}
         raw = {}
         factor_in = {}
-        grouped_out = {}
-        for s in range(-2, TILES + GROUP):
-            if s + 2 < TILES:
-                i = s + 2
-                if i % GROUP == 0:
-                    p2_group = work.tile([P, BLOCKS, GROUP, P], F32)
-                raw[i] = compare(i, upright_in[i][0], upright_in[i][2], p2_group[:, :, i % GROUP, :])
-                if i % GROUP == GROUP - 1:
-                    store(out_3, p2_group, i // GROUP)
-            if s + 3 < TILES:
-                upright_in[s + 3] = project(s + 3)
+        num_den = {}
+        wkv_in = {}
+        to_invert = []
+        to_finish = []
+
+        def logarithm(i, count=1):
+            den_done = num_den[i // GROUP][1][:, i % GROUP : i % GROUP + count]
+            nc.scalar.activation(out=den_done, in_=den_done, func=FUNC.Ln)
+
+        def invert(i):
+            den_done = num_den[i // GROUP][1][:, i % GROUP]
+            nc.scalar.activation(out=den_done, in_=den_done, func=FUNC.Exp, scale=-1.0)
+
+        def finish(i, engine):
+            num_done, den_done = num_den[i // GROUP]
+            if i % PAIR == 0:
+                wkv_pair = arena.tile([P, BLOCKS, PAIR, P], F32, bufs=4, offset=AT_PLANES)
+                wkv_in[i // PAIR] = wkv_pair
+            engine.tensor_tensor(
+                out=wkv_in[i // PAIR][:, :, i % PAIR, :],
+                in0=num_done[:, i % GROUP],
+                in1=den_done[:, i % GROUP],
+                op=ALU.mult,
+            )
+            if i % PAIR == PAIR - 1:
+                store(out_0, wkv_in[i // PAIR], i - PAIR + 1)
+
+        for s in range(-AHEAD, TILES):
+            i = s + AHEAD
+            if i < TILES:
+                if i % PAIR == 0:
+                    p2_pair = arena.tile([P, BLOCKS, PAIR, P], F32, bufs=2, offset=AT_P2)
+                raw[i] = compare(i, k_in[i], decayed_in[i], p2_pair[:, :, i % PAIR, :])
+                if i % PAIR == PAIR - 1:
+                    store(out_3, p2_pair, i - PAIR + 1)
+            for job, *args in early_jobs.get(s, []):
+                job(*args)
+            if i + 1 < TILES:
+                k_in[i + 1] = project_k(i + 1)
+            if i + SUM_AHEAD < TILES:
+                decayed_in[i + SUM_AHEAD] = decay_state(i + SUM_AHEAD)
+            if 0 <= s + 2 < TILES:
+                v_in[s + 2] = project_v(s + 2)
+            for done in to_finish:
+                finish(done, nc.gpsimd)
+            to_finish = []
             if 0 <= s < TILES:
+                m = s % PAIR
                 n = s % GROUP
+                if m == 0:
+                    aa_pair = arena.tile([P, BLOCKS, PAIR, P], F32, bufs=2, offset=AT_AA)
+                    bb_pair = arena.tile([P, BLOCKS, PAIR, P], F32, bufs=2, offset=AT_BB)
                 if n == 0:
-                    aa_group = work.tile([P, BLOCKS, GROUP, P], F32)
-                    bb_group = work.tile([P, BLOCKS, GROUP, P], F32)
-                    num_group = work.tile([P, BLOCKS, GROUP, P], F32)
-                    den_group = work.tile([P, BLOCKS, GROUP, P], F32)
-                    grouped_out[s // GROUP] = (num_group, den_group)
+                    odd = (s // GROUP) % 2
+                    at = (AT_QUOTIENT, AT_WEIGHTS_1)[odd]
+                    num_group = arena.tile([P, GROUP, BLOCKS, P], F32, name=f"num{odd}", offset=at)
+                    den_group = arena.tile(
+                        [P, GROUP, BLOCKS, P], F32, name=f"den{odd}", offset=at + 2 * CHUNK
+                    )
+                    num_den[s // GROUP] = (num_group, den_group)
                 blend(
                     s,
                     factor_in[s],
-                    upright_in[s][1],
-                    aa_group[:, :, n, :],
-                    bb_group[:, :, n, :],
-                    num_group[:, :, n, :],
-                    den_group[:, :, n, :],
+                    v_in[s],
+                    aa_pair[:, :, m, :],
+                    bb_pair[:, :, m, :],
+                    num_group[:, n],
+                    den_group[:, n],
+                    nc.vector if s == TILES - 1 else nc.gpsimd,
                 )
-                if n == GROUP - 1:
-                    store(out_1, aa_group, s // GROUP)
-                    store(out_2, bb_group, s // GROUP)
+                if m == PAIR - 1:
+                    store(out_2, bb_pair, s - PAIR + 1)
+                    store(out_1, aa_pair, s - PAIR + 1)
             if 0 <= s + 1 < TILES:
                 factor_in[s + 1] = [
                     upright(raw[s + 1][n], name) for n, name in enumerate(FACTOR_BANKS)
                 ]
-            if s >= GROUP:
-                q = s // GROUP - 1
-                b = s % GROUP
-                num_done, den_done = grouped_out[q]
-                if b == 0:
-                    nc.scalar.activation(out=den_done[:], in_=den_done[:], func=FUNC.Ln)
-                nc.scalar.activation(out=den_done[:, b], in_=den_done[:, b], func=FUNC.Exp, scale=-1.0)
-                wkv_rows = work.tile([P, GROUP, P], F32, bufs=3)
-                nc.gpsimd.tensor_tensor(
-                    out=wkv_rows[:], in0=num_done[:, b], in1=den_done[:, b], op=ALU.mult
-                )
-                nc.sync.dma_start(
-                    out=out_0[rows_of(q * GROUP, b, 1), cols_of(q * GROUP, GROUP)],
-                    in_=wkv_rows[:].rearrange("p n c -> p (n c)"),
-                )
+            for extra in range(2 if s == TILES - AHEAD else 1):
+                if to_invert:
+                    if to_invert[0] % GROUP == 0:
+                        logarithm(to_invert[0], GROUP)
+                    invert(to_invert[0])
+                    to_finish.append(to_invert.pop(0))
+            if s >= 0 and s % GROUP == GROUP - 1 and s < TILES - 1:
+                to_invert += range(s - GROUP + 1, s + 1)
+            if s == TILES - AHEAD:
+                for done in range(TILES - GROUP, s):
+                    logarithm(done)
+            if s >= TILES - AHEAD:
+                logarithm(s)
+            for job, *args in late_jobs.get(s, []):
+                job(*args)
+        for done in to_finish:
+            finish(done, nc.gpsimd)
+        for done in range(TILES - GROUP, TILES):
+            invert(done)
+            finish(done, nc.vector)

@@ -41,6 +41,7 @@ AT_AA = AT_HIDDEN_0 + 2 * CHUNK
 AT_BB = AT_WEIGHTS_0
 AT_P1 = AT_WEIGHTS_0 + 2 * CHUNK
 AT_QUOTIENT = 26 * CHUNK
+BY_DIFFERENCE = ((0, 0, 0), (0, 0, 1), (0, 1, 0), (0, 1, 1), (1, 0, 0), (1, 0, 1))
 E_CAP = 2.0**60
 AHEAD = 2
 SUM_AHEAD = 7
@@ -111,6 +112,7 @@ def tile_rwkv_attention_pa_kernel(
         wv_scales = keep.tile([P, PASSES, WIDTH], U8, align_bytes=64)
         decay_rows = keep.tile([P, WIDTH], BF16)
         ident = keep.tile([P, P], BF16)
+        minus_ident = keep.tile([P, P], BF16)
         ident_f32 = keep.tile([P, P], F32)
         vector_rows = keep.tile([P, K_PASS], BF16)
         columns = keep.tile([P, 4 * CHUNKS], F32)
@@ -126,16 +128,56 @@ def tile_rwkv_attention_pa_kernel(
         def half_of(source, h):
             return source.rearrange("(h r p) d -> h p r d", r=BLOCKS, p=P)[h]
 
+        def turn_words(bank, rows, u):
+            words = rows[:].bitcast(F32)
+            for b in range(BLOCKS):
+                nc.tensor.transpose(
+                    bank[:, b * P : (b + 1) * P], words[:, b, u : K_PASS // 2 : 2], ident_f32[:]
+                )
+
+        def turn_difference(bank, x_rows, s_rows, t):
+            for b in range(BLOCKS):
+                for rows, sign in ((x_rows, ident), (s_rows, minus_ident)):
+                    nc.tensor.matmul(
+                        bank[:, b * P : (b + 1) * P],
+                        lhsT=rows[:, b, t:K_PASS:PACK],
+                        rhs=sign[:],
+                        start=(sign is ident),
+                        stop=(sign is minus_ident),
+                    )
+
+        def mix_turned_words(h, g, u, pool):
+            x_rows, s_rows = hidden_of[h, g]
+            s_turned = pool.tile([P, N_TILE], F32, name="s_turned")
+            turn_words(s_turned, s_rows, u)
+            first_diff = pool.tile([P, N_TILE], F32, name="x_turned")
+            turn_difference(first_diff, x_rows, s_rows, 2 * u)
+            s_words = arena.tile([P, N_TILE], F32, bufs=4, offset=AT_OLD, name="old_part")
+            nc.scalar.copy(out=s_words[:], in_=s_turned[:])
+            second_diff = pool.tile([P, N_TILE], F32, name="s_turned")
+            turn_difference(second_diff, x_rows, s_rows, 2 * u + 1)
+            pair_of[h, g, u] = (s_words[:].bitcast(BF16), (first_diff, second_diff))
+
+        def add_difference(h, g, u):
+            old, diffs = pair_of[h, g, u]
+            for e in range(2):
+                t = 2 * u + e
+                c = g * PACK + t
+                for name, col in (("xk", c), ("xv", CHUNKS + c)):
+                    nc.vector.scalar_tensor_tensor(
+                        out=planes_of[name, h, g][:, t, :],
+                        in0=diffs[e][:],
+                        scalar=mix[:, col : col + 1],
+                        in1=old[:, e::2],
+                        op0=ALU.mult,
+                        op1=ALU.add,
+                    )
+
         def turn_pair(pool, g, u, x_rows, s_rows):
-            picked = slice(u, K_PASS // 2, 2)
             s_turned = pool.tile([P, N_TILE], F32, name="s_turned")
             x_turned = pool.tile([P, N_TILE], F32, name="x_turned")
-            for bank, rows in ((s_turned, s_rows), (x_turned, x_rows)):
-                words = rows[:].bitcast(F32)
-                for b in range(BLOCKS):
-                    nc.tensor.transpose(
-                        bank[:, b * P : (b + 1) * P], words[:, b, picked], ident_f32[:]
-                    )
+            turn_words(s_turned, s_rows, u)
+            turn_words(x_turned, x_rows, u)
             return s_turned, x_turned
 
         def scale_pair(g, u, s_turned):
@@ -186,9 +228,14 @@ def tile_rwkv_attention_pa_kernel(
             hidden_of[h, g] = (x_rows, s_rows)
 
         def turn(pool, h, g, u):
+            if (h, g, u) in BY_DIFFERENCE:
+                mix_turned_words(h, g, u, pool)
+                return
             pair_of[h, g, u] = turn_pair(pool, g, u, *hidden_of[h, g])
 
         def scale(h, g, u):
+            if (h, g, u) in BY_DIFFERENCE:
+                return
             s_turned, x_turned = pair_of[h, g, u]
             pair_of[h, g, u] = (x_turned, scale_pair(g, u, s_turned))
 
@@ -197,6 +244,9 @@ def tile_rwkv_attention_pa_kernel(
                 for name in ("xk", "xv"):
                     planes = arena.tile([P, PACK, N_TILE], BF16, bufs=4, offset=AT_PLANES)
                     planes_of[name, h, g] = planes[:]
+            if (h, g, u) in BY_DIFFERENCE:
+                add_difference(h, g, u)
+                return
             add_pair(g, u, *pair_of[h, g, u], planes_of["xk", h, g], planes_of["xv", h, g])
 
         def regroup(name, h, g, shares):
@@ -251,6 +301,7 @@ def tile_rwkv_attention_pa_kernel(
 
             make_identity(nc, ident[:])
             make_identity(nc, ident_f32[:])
+            nc.vector.tensor_scalar_mul(out=minus_ident[:], in0=ident[:], scalar1=-1.0)
             mix_turned = turned.tile([P, PACK, P], BF16, tag="x_turned")
             shift_turned = turned.tile([P, PACK, P], BF16, tag="s_turned")
             for t in range(PACK):
@@ -273,37 +324,32 @@ def tile_rwkv_attention_pa_kernel(
             nc.vector.tensor_tensor(out=shift[:], in0=decay, in1=first, op=ALU.add)
 
             V, S, G = (512, 0, 0), (0, 512, 0), (0, 0, 512)
-            regroup("wk", 0, 0, G)
-            regroup("wv", 0, 0, G)
             turn(turned, 0, 0, 0)
             turn(turned_first, 0, 0, 1)
-            scale(0, 0, 0)
             add(0, 0, 0)
             turn(turned, 0, 1, 0)
-            scale(0, 0, 1)
+            regroup("wk", 0, 0, S)
             add(0, 0, 1)
             turn(turned_first, 0, 1, 1)
-            scale(0, 1, 0)
+            regroup("wv", 0, 0, S)
             add(0, 1, 0)
             regroup("xk", 0, 0, S)
             pack("wk", 0, 0)
-            pack("wv", 0, 0)
-            regroup("wk", 0, 1, G)
-            regroup("wv", 0, 1, G)
-            scale(0, 1, 1)
             add(0, 1, 1)
-            pack("xk", 0, 0)
             regroup("xv", 0, 0, S)
+            pack("wv", 0, 0)
             regroup("xk", 0, 1, V)
-            pack("wk", 0, 1)
+            pack("xk", 0, 0)
+            regroup("wk", 0, 1, S)
             regroup("xv", 0, 1, V)
             pack("xk", 0, 1)
-            pack("wv", 0, 1)
-            turn(turned, 1, 0, 0)
             pack("xv", 0, 0)
+            regroup("wv", 0, 1, S)
+            pack("wk", 0, 1)
             pack("xv", 0, 1)
+            turn(turned, 1, 0, 0)
+            pack("wv", 0, 1)
             regroup("wk", 1, 0, S)
-            scale(1, 0, 0)
 
         banks = pools.enter_context(tc.psum_pool(name="banks", bufs=1, reuse_waits="tile"))
         p1_rows = arena.tile([P, BLOCKS, WIDTH], BF16, offset=AT_P1)
@@ -420,15 +466,14 @@ def tile_rwkv_attention_pa_kernel(
 
         early_jobs = {
 
-            0: [(scale, 1, 0, 1)],
             1: [(scale, 1, 1, 0)],
             2: [(scale, 1, 1, 1)],
         }
         late_jobs = {
 
             -2: [(regroup, "wv", 1, 0, V), (pack, "wk", 1, 0)],
-            -1: [(add, 1, 0, 0), (pack, "wv", 1, 0), (turn, turned, 1, 0, 1), (regroup, "wk", 1, 1, S)],
-            0: [(regroup, "wv", 1, 1, V), (pack, "wk", 1, 1), (add, 1, 0, 1), (pack, "wv", 1, 1), (turn, turned, 1, 1, 0), (regroup, "xk", 1, 0, S)],
+            -1: [(add, 1, 0, 0), (pack, "wv", 1, 0), (turn, turned, 1, 0, 1), (regroup, "wk", 1, 1, S), (regroup, "wv", 1, 1, S)],
+            0: [(add, 1, 0, 1), (pack, "wk", 1, 1), (pack, "wv", 1, 1), (turn, turned, 1, 1, 0), (regroup, "xk", 1, 0, S)],
             1: [(add, 1, 1, 0), (pack, "xk", 1, 0), (turn, turned, 1, 1, 1), (regroup, "xv", 1, 0, S)],
             2: [(load_second_state,), (add, 1, 1, 1), (pack, "xv", 1, 0), (regroup, "xk", 1, 1, S)],
             3: [(pack, "xk", 1, 1), (regroup, "xv", 1, 1, S)],
@@ -517,14 +562,12 @@ def tile_rwkv_attention_pa_kernel(
                 factor_in[s + 1] = [
                     upright(raw[s + 1][n], name) for n, name in enumerate(FACTOR_BANKS)
                 ]
-            for extra in range(2 if s == TILES - AHEAD else 1):
-                if to_invert:
-                    if to_invert[0] % GROUP == 0:
-                        logarithm(to_invert[0], GROUP)
-                    invert(to_invert[0])
-                    to_finish.append(to_invert.pop(0))
             if s >= 0 and s % GROUP == GROUP - 1 and s < TILES - 1:
                 to_invert += range(s - GROUP + 1, s + 1)
+                logarithm(s - GROUP + 1, GROUP)
+            if to_invert:
+                invert(to_invert[0])
+                to_finish.append(to_invert.pop(0))
             if s == TILES - AHEAD:
                 for done in range(TILES - GROUP, s):
                     logarithm(done)

@@ -44,6 +44,8 @@ AT_QUOTIENT = 26 * CHUNK
 BY_DIFFERENCE = ((0, 0, 0), (0, 0, 1), (0, 1, 0), (0, 1, 1), (1, 0, 0), (1, 0, 1))
 E_CAP = 2.0**60
 AHEAD = 2
+FIRST_SUMS = 4
+DOUBLE_SUMS = (1, 2, 3)
 SUM_AHEAD = 7
 
 FLOPS = 2 * 2 * ROWS * DEPTH * WIDTH
@@ -121,12 +123,11 @@ def tile_rwkv_attention_pa_kernel(
         mix = columns[:, 0 : 2 * CHUNKS]
         decay = columns[:, 2 * CHUNKS : 3 * CHUNKS]
         first = columns[:, 3 * CHUNKS : 4 * CHUNKS]
-        p0_rows = keep.tile([P, BLOCKS, WIDTH], BF16)
         a0_rows = keep.tile([P, BLOCKS, WIDTH], BF16)
         b0_rows = keep.tile([P, BLOCKS, WIDTH], BF16)
 
         def half_of(source, h):
-            return source.rearrange("(h r p) d -> h p r d", r=BLOCKS, p=P)[h]
+            return source.rearrange("(h p r) d -> h p r d", r=BLOCKS, p=P)[h]
 
         def turn_words(bank, rows, u):
             words = rows[:].bitcast(F32)
@@ -268,7 +269,7 @@ def tile_rwkv_attention_pa_kernel(
 
             nc.vector.memset(vector_rows[:], 0.0)
             for n, vector in enumerate((k_mixed, v_mixed, time_decay, time_first)):
-                nc.sync.dma_start(
+                nc.scalar.dma_start(
                     out=vector_rows[n * PASSES : (n + 1) * PASSES, :],
                     in_=vector.rearrange("(g k) -> g k", k=K_PASS),
                 )
@@ -290,12 +291,16 @@ def tile_rwkv_attention_pa_kernel(
             for g in range(PASSES):
                 load_hidden(0, g)
                 load_weights(0, g)
-            nc.sync.dma_start(out=decay_rows[:], in_=time_decay.partition_broadcast(P))
-            nc.sync.dma_start(out=p0_rows[:], in_=half_of(saved_p, 0))
+            p0_rows = {}
+            for c in range(COL_HALVES):
+                part = keep.tile([P, BLOCKS, N_TILE], BF16, name=f"p0{c}")
+                p0_rows[c] = part
+            nc.sync.dma_start(out=p0_rows[0][:], in_=half_of(saved_p, 0)[:, :, 0:N_TILE])
             load_hidden(1, 0)
-            for g in range(PASSES):
-                load_weights(1, g)
+            load_weights(1, 0)
+            load_weights(1, 1)
             load_hidden(1, 1)
+            nc.sync.dma_start(out=p0_rows[1][:], in_=half_of(saved_p, 0)[:, :, N_TILE:WIDTH])
             nc.sync.dma_start(out=a0_rows[:], in_=half_of(saved_a, 0))
             nc.sync.dma_start(out=b0_rows[:], in_=half_of(saved_b, 0))
 
@@ -326,6 +331,15 @@ def tile_rwkv_attention_pa_kernel(
             V, S, G = (512, 0, 0), (0, 512, 0), (0, 0, 512)
             turn(turned, 0, 0, 0)
             turn(turned_first, 0, 0, 1)
+            for c, name in enumerate(("k_ps", "v_ps")):
+                spread = early.tile([P, N_TILE], F32, name=name)
+                for j in range(BLOCKS):
+                    nc.tensor.transpose(
+                        spread[:, j * P : (j + 1) * P],
+                        decay[:, c * BLOCKS + j : c * BLOCKS + j + 1].to_broadcast([P, P]),
+                        ident_f32[:],
+                    )
+                nc.scalar.copy(out=decay_rows[:, c * N_TILE : (c + 1) * N_TILE], in_=spread[:])
             add(0, 0, 0)
             turn(turned, 0, 1, 0)
             regroup("wk", 0, 0, S)
@@ -354,7 +368,6 @@ def tile_rwkv_attention_pa_kernel(
         banks = pools.enter_context(tc.psum_pool(name="banks", bufs=1, reuse_waits="tile"))
         p1_rows = arena.tile([P, BLOCKS, WIDTH], BF16, offset=AT_P1)
         nc.sync.dma_start(out=p1_rows[:], in_=half_of(saved_p, 1))
-        p_halves = [p0_rows, p1_rows]
         a_halves = [a0_rows]
         b_halves = [b0_rows]
 
@@ -369,9 +382,6 @@ def tile_rwkv_attention_pa_kernel(
         def rows_of(i, b=0, count=BLOCKS):
             first_row = (i // COL_BLOCKS) * N_TILE + b * P
             return slice(first_row, first_row + count * P)
-
-        def blocks_of(i):
-            return slice((i // COL_BLOCKS) * BLOCKS, (i // COL_BLOCKS + 1) * BLOCKS)
 
         def cols_of(i, count=1):
             return slice((i % COL_BLOCKS) * P, (i % COL_BLOCKS + count) * P)
@@ -401,7 +411,11 @@ def tile_rwkv_attention_pa_kernel(
             decayed = work.tile([P, BLOCKS, P], F32, bufs=SUM_AHEAD + 1)
             nc.gpsimd.tensor_tensor(
                 out=decayed[:],
-                in0=part_of(p_halves, i),
+                in0=(
+                    p1_rows[:, :, cols_of(i)]
+                    if i >= COL_BLOCKS
+                    else p0_rows[i * P // N_TILE][:, :, i * P % N_TILE : i * P % N_TILE + P]
+                ),
                 in1=decay_rows[:, cols_of(i)].unsqueeze(1).to_broadcast([P, BLOCKS, P]),
                 op=ALU.add,
             )
@@ -460,29 +474,33 @@ def tile_rwkv_attention_pa_kernel(
 
         def store(out, pair_tile, i):
             nc.sync.dma_start(
-                out=out.rearrange("(r p) a -> p r a", p=P)[:, blocks_of(i), cols_of(i, PAIR)],
+                out=half_of(out, i // COL_BLOCKS)[:, :, cols_of(i, PAIR)],
                 in_=pair_tile[:].rearrange("p b n c -> p b (n c)"),
             )
 
         early_jobs = {
 
-            1: [(scale, 1, 1, 0)],
-            2: [(scale, 1, 1, 1)],
+            -1: [(pack, "wk", 1, 0)],
+            0: [(pack, "wv", 1, 0)],
+            1: [(pack, "wk", 1, 1), (pack, "wv", 1, 1), (scale, 1, 1, 0)],
+            2: [(pack, "xk", 1, 0), (scale, 1, 1, 1)],
+            3: [(pack, "xv", 1, 0)],
+            4: [(pack, "xk", 1, 1)],
+            5: [(pack, "xv", 1, 1)],
         }
         late_jobs = {
 
-            -2: [(regroup, "wv", 1, 0, V), (pack, "wk", 1, 0)],
-            -1: [(add, 1, 0, 0), (pack, "wv", 1, 0), (turn, turned, 1, 0, 1), (regroup, "wk", 1, 1, S), (regroup, "wv", 1, 1, S)],
-            0: [(add, 1, 0, 1), (pack, "wk", 1, 1), (pack, "wv", 1, 1), (turn, turned, 1, 1, 0), (regroup, "xk", 1, 0, S)],
-            1: [(add, 1, 1, 0), (pack, "xk", 1, 0), (turn, turned, 1, 1, 1), (regroup, "xv", 1, 0, S)],
-            2: [(load_second_state,), (add, 1, 1, 1), (pack, "xv", 1, 0), (regroup, "xk", 1, 1, S)],
-            3: [(pack, "xk", 1, 1), (regroup, "xv", 1, 1, S)],
-            4: [(pack, "xv", 1, 1)],
+            -2: [(regroup, "wv", 1, 0, V)],
+            -1: [(add, 1, 0, 0), (turn, turned, 1, 0, 1), (regroup, "wk", 1, 1, S), (regroup, "wv", 1, 1, S)],
+            0: [(add, 1, 0, 1), (turn, turned, 1, 1, 0), (regroup, "xk", 1, 0, S)],
+            1: [(add, 1, 1, 0), (turn, turned, 1, 1, 1), (regroup, "xv", 1, 0, S)],
+            2: [(load_second_state,), (add, 1, 1, 1), (regroup, "xk", 1, 1, S)],
+            3: [(regroup, "xv", 1, 1, S)],
         }
 
         k_in = {0: project_k(0)}
         v_in = {}
-        decayed_in = {i: decay_state(i) for i in range(SUM_AHEAD)}
+        decayed_in = {i: decay_state(i) for i in range(FIRST_SUMS)}
         raw = {}
         factor_in = {}
         num_den = {}
@@ -524,8 +542,9 @@ def tile_rwkv_attention_pa_kernel(
                 job(*args)
             if i + 1 < TILES:
                 k_in[i + 1] = project_k(i + 1)
-            if i + SUM_AHEAD < TILES:
-                decayed_in[i + SUM_AHEAD] = decay_state(i + SUM_AHEAD)
+            for extra in range(2 if s in DOUBLE_SUMS else 1):
+                if len(decayed_in) < TILES:
+                    decayed_in[len(decayed_in)] = decay_state(len(decayed_in))
             if 0 <= s + 2 < TILES:
                 v_in[s + 2] = project_v(s + 2)
             for done in to_finish:

@@ -25,7 +25,6 @@ COL_HALVES = WIDTH // N_TILE
 BLOCKS = N_TILE // P
 COL_BLOCKS = WIDTH // P
 TILES = ROW_HALVES * COL_BLOCKS
-FACTOR_BANKS = ("e_ps", "f1_ps", "f2_ps")
 GROUP = 4
 PAIR = 2
 CHUNK = PACK * N_TILE * 2
@@ -44,6 +43,7 @@ AT_QUOTIENT = 26 * CHUNK
 BY_DIFFERENCE = ((0, 0, 0), (0, 0, 1), (0, 1, 0), (0, 1, 1), (1, 0, 0), (1, 0, 1))
 E_CAP = 2.0**60
 AHEAD = 2
+WARM_STEPS = range(3, 14)
 FIRST_SUMS = 4
 DOUBLE_SUMS = (1, 2, 3)
 SUM_AHEAD = 7
@@ -219,12 +219,14 @@ def tile_rwkv_attention_pa_kernel(
         pair_of = {}
         hidden_of = {}
 
-        def load_hidden(h, g):
+        def load_hidden(h, g, between=None):
             depth = slice(g * K_PASS, (g + 1) * K_PASS)
             at = (AT_HIDDEN_0, AT_HIDDEN_1)[h] + 2 * g * CHUNK
             s_rows = arena.tile([P, BLOCKS, K_PASS], BF16, name=f"s{h}{g}", offset=at)
             x_rows = arena.tile([P, BLOCKS, K_PASS], BF16, name=f"x{h}{g}", offset=at + CHUNK)
             nc.sync.dma_start(out=s_rows[:], in_=half_of(saved_x, h)[:, :, depth])
+            if between is not None:
+                between()
             nc.sync.dma_start(out=x_rows[:], in_=half_of(x, h)[:, :, depth])
             hidden_of[h, g] = (x_rows, s_rows)
 
@@ -268,17 +270,10 @@ def tile_rwkv_attention_pa_kernel(
             turned_first = first_pools.enter_context(tc.psum_pool(name="turned_first", bufs=1))
 
             nc.vector.memset(vector_rows[:], 0.0)
-            for n, vector in enumerate((k_mixed, v_mixed, time_decay, time_first)):
-                nc.scalar.dma_start(
-                    out=vector_rows[n * PASSES : (n + 1) * PASSES, :],
-                    in_=vector.rearrange("(g k) -> g k", k=K_PASS),
-                )
             w_views = {
                 "wk": key_weight.rearrange("(g p t) a -> g p t a", t=PACK, p=P),
                 "wv": value_weight.rearrange("(g p t) a -> g p t a", t=PACK, p=P),
             }
-            w_planes = {}
-
             def load_weights(c, g):
                 for name in ("wk", "wv"):
                     at = (AT_WEIGHTS_0, AT_WEIGHTS_1)[c] + (2 * g + (name == "wv")) * CHUNK
@@ -288,9 +283,17 @@ def tile_rwkv_attention_pa_kernel(
                     )
                     planes_of[name, c, g] = planes[:]
 
-            for g in range(PASSES):
-                load_hidden(0, g)
-                load_weights(0, g)
+            def load_vectors():
+                for n, vector in enumerate((k_mixed, v_mixed, time_decay, time_first)):
+                    nc.sync.dma_start(
+                        out=vector_rows[n * PASSES : (n + 1) * PASSES, :],
+                        in_=vector.rearrange("(g k) -> g k", k=K_PASS),
+                    )
+
+            load_hidden(0, 0, between=load_vectors)
+            load_weights(0, 0)
+            load_hidden(0, 1)
+            load_weights(0, 1)
             p0_rows = {}
             for c in range(COL_HALVES):
                 part = keep.tile([P, BLOCKS, N_TILE], BF16, name=f"p0{c}")
@@ -421,6 +424,10 @@ def tile_rwkv_attention_pa_kernel(
             )
             return decayed
 
+        def keep_warm(i):
+            idle_bank = early.tile([P, BLOCKS, P], F32, name="lead_turned")
+            project(i, idle_bank, xv_codes, xv_scales, wv_codes, wv_scales)
+
         def project_v(i):
             v_ps = early.tile([P, BLOCKS, P], F32)
             project(i, v_ps, xv_codes, xv_scales, wv_codes, wv_scales)
@@ -433,7 +440,7 @@ def tile_rwkv_attention_pa_kernel(
             lead = work.tile([P, BLOCKS, P], F32)
             nc.vector.tensor_tensor(out=lead[:], in0=k_ps[:], in1=decayed[:], op=ALU.subtract)
             nc.vector.tensor_tensor(out=p2, in0=k_ps[:], in1=decayed[:], op=ALU.max)
-            lead_turned = early.tile([P, N_TILE], F32)
+            lead_turned = early.tile([P, N_TILE], F32, name="lead_turned")
             for b in range(BLOCKS):
                 nc.tensor.transpose(lead_turned[:, b * P : (b + 1) * P], lead[:, b, :], ident_f32[:])
             e_raw = work.tile([P, N_TILE], F32, bufs=AHEAD)
@@ -457,17 +464,19 @@ def tile_rwkv_attention_pa_kernel(
                 out=out, in0=raw[:], scalar=cap, in1=other, op0=ALU.min, op1=op
             )
 
-        def blend(i, factor_banks, v_rows, aa, bb, num, den, adder):
-            e_ps, f1_ps, f2_ps = factor_banks
-            a_part = part_of(a_halves, i)
-            b_part = part_of(b_halves, i)
-            f1_a = work.tile([P, BLOCKS, P], F32)
-            f2_v = work.tile([P, BLOCKS, P], F32)
+        def quotient(i, e_ps, v_rows, num, den):
             clamped(num, e_ps, v_rows[:], ALU.mult, E_CAP)
-            clamped(den, e_ps, b_part, ALU.add, E_CAP)
-            nc.gpsimd.tensor_tensor(out=num, in0=num, in1=a_part, op=ALU.add)
-            clamped(f1_a[:], f1_ps, a_part, ALU.mult)
-            clamped(bb, f1_ps, b_part, ALU.mult)
+            clamped(den, e_ps, part_of(b_halves, i), ALU.add, E_CAP)
+            nc.gpsimd.tensor_tensor(out=num, in0=num, in1=part_of(a_halves, i), op=ALU.add)
+
+        def keep_state(i, f1_ps, bb):
+            f1_a = work.tile([P, BLOCKS, P], F32)
+            clamped(f1_a[:], f1_ps, part_of(a_halves, i), ALU.mult)
+            clamped(bb, f1_ps, part_of(b_halves, i), ALU.mult)
+            return f1_a
+
+        def add_token(f2_ps, f1_a, v_rows, aa, bb, adder):
+            f2_v = work.tile([P, BLOCKS, P], F32)
             clamped(f2_v[:], f2_ps, v_rows[:], ALU.mult)
             clamped(bb, f2_ps, bb, ALU.add)
             adder.tensor_tensor(out=aa, in0=f1_a[:], in1=f2_v[:], op=ALU.add)
@@ -542,15 +551,17 @@ def tile_rwkv_attention_pa_kernel(
                 job(*args)
             if i + 1 < TILES:
                 k_in[i + 1] = project_k(i + 1)
+            if 0 <= s + 2 < TILES:
+                v_in[s + 2] = project_v(s + 2)
             for extra in range(2 if s in DOUBLE_SUMS else 1):
                 if len(decayed_in) < TILES:
                     decayed_in[len(decayed_in)] = decay_state(len(decayed_in))
-            if 0 <= s + 2 < TILES:
-                v_in[s + 2] = project_v(s + 2)
             for done in to_finish:
                 finish(done, nc.gpsimd)
             to_finish = []
-            if 0 <= s < TILES:
+            blends = 0 <= s < TILES
+            follows = 0 <= s + 1 < TILES
+            if blends:
                 m = s % PAIR
                 n = s % GROUP
                 if m == 0:
@@ -564,23 +575,26 @@ def tile_rwkv_attention_pa_kernel(
                         [P, GROUP, BLOCKS, P], F32, name=f"den{odd}", offset=at + 2 * CHUNK
                     )
                     num_den[s // GROUP] = (num_group, den_group)
-                blend(
-                    s,
-                    factor_in[s],
-                    v_in[s],
-                    aa_pair[:, :, m, :],
-                    bb_pair[:, :, m, :],
-                    num_group[:, n],
-                    den_group[:, n],
-                    nc.vector if s == TILES - 1 else nc.gpsimd,
+                aa = aa_pair[:, :, m, :]
+                bb = bb_pair[:, :, m, :]
+                quotient(s, factor_in[s, 0], v_in[s], num_group[:, n], den_group[:, n])
+            if follows:
+                factor_in[s + 1, 0] = upright(raw[s + 1][0], "e_ps")
+            if blends:
+                f1_a = keep_state(s, factor_in[s, 1], bb)
+            if follows:
+                factor_in[s + 1, 1] = upright(raw[s + 1][1], "f1_ps")
+            if s in WARM_STEPS:
+                keep_warm(s)
+            if blends:
+                add_token(
+                    factor_in[s, 2], f1_a, v_in[s], aa, bb, nc.vector if s == TILES - 1 else nc.gpsimd
                 )
                 if m == PAIR - 1:
                     store(out_2, bb_pair, s - PAIR + 1)
                     store(out_1, aa_pair, s - PAIR + 1)
-            if 0 <= s + 1 < TILES:
-                factor_in[s + 1] = [
-                    upright(raw[s + 1][n], name) for n, name in enumerate(FACTOR_BANKS)
-                ]
+            if follows:
+                factor_in[s + 1, 2] = upright(raw[s + 1][2], "f2_ps")
             if s >= 0 and s % GROUP == GROUP - 1 and s < TILES - 1:
                 to_invert += range(s - GROUP + 1, s + 1)
                 logarithm(s - GROUP + 1, GROUP)

@@ -43,7 +43,6 @@ AT_QUOTIENT = 26 * CHUNK
 BY_DIFFERENCE = ((0, 0, 0), (0, 0, 1), (0, 1, 0), (0, 1, 1), (1, 0, 0), (1, 0, 1))
 E_CAP = 2.0**60
 AHEAD = 2
-WARM_STEPS = range(3, 14)
 FIRST_SUMS = 4
 DOUBLE_SUMS = (1, 2, 3)
 SUM_AHEAD = 7
@@ -130,7 +129,7 @@ def tile_rwkv_attention_pa_kernel(
             return source.rearrange("(h p r) d -> h p r d", r=BLOCKS, p=P)[h]
 
         def turn_words(bank, rows, u):
-            words = rows[:].bitcast(F32)
+            words = rows.bitcast(F32)
             for b in range(BLOCKS):
                 nc.tensor.transpose(
                     bank[:, b * P : (b + 1) * P], words[:, b, u : K_PASS // 2 : 2], ident_f32[:]
@@ -219,16 +218,25 @@ def tile_rwkv_attention_pa_kernel(
         pair_of = {}
         hidden_of = {}
 
-        def load_hidden(h, g, between=None):
+        def load_first_hidden(g, between=None):
             depth = slice(g * K_PASS, (g + 1) * K_PASS)
-            at = (AT_HIDDEN_0, AT_HIDDEN_1)[h] + 2 * g * CHUNK
-            s_rows = arena.tile([P, BLOCKS, K_PASS], BF16, name=f"s{h}{g}", offset=at)
-            x_rows = arena.tile([P, BLOCKS, K_PASS], BF16, name=f"x{h}{g}", offset=at + CHUNK)
-            nc.sync.dma_start(out=s_rows[:], in_=half_of(saved_x, h)[:, :, depth])
+            at = AT_HIDDEN_0 + 2 * g * CHUNK
+            s_rows = arena.tile([P, BLOCKS, K_PASS], BF16, name=f"s0{g}", offset=at)
+            x_rows = arena.tile([P, BLOCKS, K_PASS], BF16, name=f"x0{g}", offset=at + CHUNK)
+            nc.sync.dma_start(out=s_rows[:], in_=half_of(saved_x, 0)[:, :, depth])
             if between is not None:
                 between()
-            nc.sync.dma_start(out=x_rows[:], in_=half_of(x, h)[:, :, depth])
-            hidden_of[h, g] = (x_rows, s_rows)
+            nc.sync.dma_start(out=x_rows[:], in_=half_of(x, 0)[:, :, depth])
+            hidden_of[0, g] = (x_rows[:], s_rows[:])
+
+        def load_second_hidden():
+            s_rows = arena.tile([P, BLOCKS, DEPTH], BF16, name="s1", offset=AT_HIDDEN_1)
+            x_rows = arena.tile([P, BLOCKS, DEPTH], BF16, name="x1", offset=AT_HIDDEN_1 + 2 * CHUNK)
+            nc.sync.dma_start(out=s_rows[:], in_=half_of(saved_x, 1))
+            nc.sync.dma_start(out=x_rows[:], in_=half_of(x, 1))
+            for g in range(PASSES):
+                depth = slice(g * K_PASS, (g + 1) * K_PASS)
+                hidden_of[1, g] = (x_rows[:, :, depth], s_rows[:, :, depth])
 
         def turn(pool, h, g, u):
             if (h, g, u) in BY_DIFFERENCE:
@@ -274,14 +282,12 @@ def tile_rwkv_attention_pa_kernel(
                 "wk": key_weight.rearrange("(g p t) a -> g p t a", t=PACK, p=P),
                 "wv": value_weight.rearrange("(g p t) a -> g p t a", t=PACK, p=P),
             }
-            def load_weights(c, g):
-                for name in ("wk", "wv"):
-                    at = (AT_WEIGHTS_0, AT_WEIGHTS_1)[c] + (2 * g + (name == "wv")) * CHUNK
-                    planes = arena.tile([P, PACK, N_TILE], BF16, name=f"{name}{c}{g}", offset=at)
-                    nc.sync.dma_start(
-                        out=planes[:], in_=w_views[name][g][:, :, c * N_TILE : (c + 1) * N_TILE]
-                    )
-                    planes_of[name, c, g] = planes[:]
+            def load_weights(name, g):
+                at = (AT_WEIGHTS_0, AT_WEIGHTS_1)[g] + (name == "wv") * 2 * CHUNK
+                planes = arena.tile([P, PACK, WIDTH], BF16, name=f"{name}{g}", offset=at)
+                nc.sync.dma_start(out=planes[:], in_=w_views[name][g])
+                for c in range(COL_HALVES):
+                    planes_of[name, c, g] = planes[:, :, c * N_TILE : (c + 1) * N_TILE]
 
             def load_vectors():
                 for n, vector in enumerate((k_mixed, v_mixed, time_decay, time_first)):
@@ -290,20 +296,24 @@ def tile_rwkv_attention_pa_kernel(
                         in_=vector.rearrange("(g k) -> g k", k=K_PASS),
                     )
 
-            load_hidden(0, 0, between=load_vectors)
-            load_weights(0, 0)
-            load_hidden(0, 1)
-            load_weights(0, 1)
             p0_rows = {}
-            for c in range(COL_HALVES):
+
+            def load_first_state(c):
                 part = keep.tile([P, BLOCKS, N_TILE], BF16, name=f"p0{c}")
+                nc.sync.dma_start(
+                    out=part[:], in_=half_of(saved_p, 0)[:, :, c * N_TILE : (c + 1) * N_TILE]
+                )
                 p0_rows[c] = part
-            nc.sync.dma_start(out=p0_rows[0][:], in_=half_of(saved_p, 0)[:, :, 0:N_TILE])
-            load_hidden(1, 0)
-            load_weights(1, 0)
-            load_weights(1, 1)
-            load_hidden(1, 1)
-            nc.sync.dma_start(out=p0_rows[1][:], in_=half_of(saved_p, 0)[:, :, N_TILE:WIDTH])
+
+            load_first_hidden(0, between=load_vectors)
+            load_first_hidden(1)
+            load_weights("wk", 0)
+            load_first_state(0)
+            load_weights("wv", 0)
+            load_weights("wk", 1)
+            load_weights("wv", 1)
+            load_second_hidden()
+            load_first_state(1)
             nc.sync.dma_start(out=a0_rows[:], in_=half_of(saved_a, 0))
             nc.sync.dma_start(out=b0_rows[:], in_=half_of(saved_b, 0))
 
@@ -345,14 +355,14 @@ def tile_rwkv_attention_pa_kernel(
                 nc.scalar.copy(out=decay_rows[:, c * N_TILE : (c + 1) * N_TILE], in_=spread[:])
             add(0, 0, 0)
             turn(turned, 0, 1, 0)
-            regroup("wk", 0, 0, S)
+            regroup("wk", 0, 0, G)
             add(0, 0, 1)
             turn(turned_first, 0, 1, 1)
             regroup("wv", 0, 0, S)
             add(0, 1, 0)
             regroup("xk", 0, 0, S)
-            pack("wk", 0, 0)
             add(0, 1, 1)
+            pack("wk", 0, 0)
             regroup("xv", 0, 0, S)
             pack("wv", 0, 0)
             regroup("xk", 0, 1, V)
@@ -369,8 +379,13 @@ def tile_rwkv_attention_pa_kernel(
             regroup("wk", 1, 0, S)
 
         banks = pools.enter_context(tc.psum_pool(name="banks", bufs=1, reuse_waits="tile"))
-        p1_rows = arena.tile([P, BLOCKS, WIDTH], BF16, offset=AT_P1)
-        nc.sync.dma_start(out=p1_rows[:], in_=half_of(saved_p, 1))
+        p1_rows = []
+
+        def load_second_p():
+            rows = arena.tile([P, BLOCKS, WIDTH], BF16, name="p1_rows", offset=AT_P1)
+            nc.sync.dma_start(out=rows[:], in_=half_of(saved_p, 1))
+            p1_rows.append(rows)
+
         a_halves = [a0_rows]
         b_halves = [b0_rows]
 
@@ -415,7 +430,7 @@ def tile_rwkv_attention_pa_kernel(
             nc.gpsimd.tensor_tensor(
                 out=decayed[:],
                 in0=(
-                    p1_rows[:, :, cols_of(i)]
+                    p1_rows[0][:, :, cols_of(i)]
                     if i >= COL_BLOCKS
                     else p0_rows[i * P // N_TILE][:, :, i * P % N_TILE : i * P % N_TILE + P]
                 ),
@@ -423,10 +438,6 @@ def tile_rwkv_attention_pa_kernel(
                 op=ALU.add,
             )
             return decayed
-
-        def keep_warm(i):
-            idle_bank = early.tile([P, BLOCKS, P], F32, name="lead_turned")
-            project(i, idle_bank, xv_codes, xv_scales, wv_codes, wv_scales)
 
         def project_v(i):
             v_ps = early.tile([P, BLOCKS, P], F32)
@@ -481,11 +492,25 @@ def tile_rwkv_attention_pa_kernel(
             clamped(bb, f2_ps, bb, ALU.add)
             adder.tensor_tensor(out=aa, in0=f1_a[:], in1=f2_v[:], op=ALU.add)
 
-        def store(out, pair_tile, i):
-            nc.sync.dma_start(
-                out=half_of(out, i // COL_BLOCKS)[:, :, cols_of(i, PAIR)],
-                in_=pair_tile[:].rearrange("p b n c -> p b (n c)"),
-            )
+        outputs = {}
+
+        def output_part(name, at, bufs, i):
+            alone = i >= TILES - PAIR
+            if alone or i % PAIR == 0:
+                tile = arena.tile(
+                    [P, BLOCKS, 1 if alone else PAIR, P], F32, name=name, bufs=bufs, offset=at
+                )
+                outputs[name] = tile
+            return outputs[name][:, :, 0 if alone else i % PAIR, :]
+
+        def store(out, name, i):
+            alone = i >= TILES - PAIR
+            if alone or i % PAIR == PAIR - 1:
+                count = 1 if alone else PAIR
+                nc.sync.dma_start(
+                    out=half_of(out, i // COL_BLOCKS)[:, :, cols_of(i - count + 1, count)],
+                    in_=outputs[name][:].rearrange("p b n c -> p b (n c)"),
+                )
 
         early_jobs = {
 
@@ -500,7 +525,7 @@ def tile_rwkv_attention_pa_kernel(
         late_jobs = {
 
             -2: [(regroup, "wv", 1, 0, V)],
-            -1: [(add, 1, 0, 0), (turn, turned, 1, 0, 1), (regroup, "wk", 1, 1, S), (regroup, "wv", 1, 1, S)],
+            -1: [(load_second_p,), (add, 1, 0, 0), (turn, turned, 1, 0, 1), (regroup, "wk", 1, 1, S), (regroup, "wv", 1, 1, S)],
             0: [(add, 1, 0, 1), (turn, turned, 1, 1, 0), (regroup, "xk", 1, 0, S)],
             1: [(add, 1, 1, 0), (turn, turned, 1, 1, 1), (regroup, "xv", 1, 0, S)],
             2: [(load_second_state,), (add, 1, 1, 1), (regroup, "xk", 1, 1, S)],
@@ -513,7 +538,6 @@ def tile_rwkv_attention_pa_kernel(
         raw = {}
         factor_in = {}
         num_den = {}
-        wkv_in = {}
         to_invert = []
         to_finish = []
 
@@ -527,26 +551,19 @@ def tile_rwkv_attention_pa_kernel(
 
         def finish(i, engine):
             num_done, den_done = num_den[i // GROUP]
-            if i % PAIR == 0:
-                wkv_pair = arena.tile([P, BLOCKS, PAIR, P], F32, bufs=4, offset=AT_PLANES)
-                wkv_in[i // PAIR] = wkv_pair
             engine.tensor_tensor(
-                out=wkv_in[i // PAIR][:, :, i % PAIR, :],
+                out=output_part("wkv", AT_PLANES, 4, i),
                 in0=num_done[:, i % GROUP],
                 in1=den_done[:, i % GROUP],
                 op=ALU.mult,
             )
-            if i % PAIR == PAIR - 1:
-                store(out_0, wkv_in[i // PAIR], i - PAIR + 1)
+            store(out_0, "wkv", i)
 
         for s in range(-AHEAD, TILES):
             i = s + AHEAD
             if i < TILES:
-                if i % PAIR == 0:
-                    p2_pair = arena.tile([P, BLOCKS, PAIR, P], F32, bufs=2, offset=AT_P2)
-                raw[i] = compare(i, k_in[i], decayed_in[i], p2_pair[:, :, i % PAIR, :])
-                if i % PAIR == PAIR - 1:
-                    store(out_3, p2_pair, i - PAIR + 1)
+                raw[i] = compare(i, k_in[i], decayed_in[i], output_part("p2", AT_P2, 2, i))
+                store(out_3, "p2", i)
             for job, *args in early_jobs.get(s, []):
                 job(*args)
             if i + 1 < TILES:
@@ -562,11 +579,7 @@ def tile_rwkv_attention_pa_kernel(
             blends = 0 <= s < TILES
             follows = 0 <= s + 1 < TILES
             if blends:
-                m = s % PAIR
                 n = s % GROUP
-                if m == 0:
-                    aa_pair = arena.tile([P, BLOCKS, PAIR, P], F32, bufs=2, offset=AT_AA)
-                    bb_pair = arena.tile([P, BLOCKS, PAIR, P], F32, bufs=2, offset=AT_BB)
                 if n == 0:
                     odd = (s // GROUP) % 2
                     at = (AT_QUOTIENT, AT_WEIGHTS_1)[odd]
@@ -575,8 +588,8 @@ def tile_rwkv_attention_pa_kernel(
                         [P, GROUP, BLOCKS, P], F32, name=f"den{odd}", offset=at + 2 * CHUNK
                     )
                     num_den[s // GROUP] = (num_group, den_group)
-                aa = aa_pair[:, :, m, :]
-                bb = bb_pair[:, :, m, :]
+                aa = output_part("aa", AT_AA, 2, s)
+                bb = output_part("bb", AT_BB, 2, s)
                 quotient(s, factor_in[s, 0], v_in[s], num_group[:, n], den_group[:, n])
             if follows:
                 factor_in[s + 1, 0] = upright(raw[s + 1][0], "e_ps")
@@ -584,15 +597,12 @@ def tile_rwkv_attention_pa_kernel(
                 f1_a = keep_state(s, factor_in[s, 1], bb)
             if follows:
                 factor_in[s + 1, 1] = upright(raw[s + 1][1], "f1_ps")
-            if s in WARM_STEPS:
-                keep_warm(s)
             if blends:
                 add_token(
                     factor_in[s, 2], f1_a, v_in[s], aa, bb, nc.vector if s == TILES - 1 else nc.gpsimd
                 )
-                if m == PAIR - 1:
-                    store(out_2, bb_pair, s - PAIR + 1)
-                    store(out_1, aa_pair, s - PAIR + 1)
+                store(out_2, "bb", s)
+                store(out_1, "aa", s)
             if follows:
                 factor_in[s + 1, 2] = upright(raw[s + 1][2], "f2_ps")
             if s >= 0 and s % GROUP == GROUP - 1 and s < TILES - 1:

@@ -35,15 +35,20 @@ AT_GROUPED = 12 * CHUNK
 AT_OLD = 16 * CHUNK
 AT_HIDDEN_0 = 18 * CHUNK
 AT_WEIGHTS_0 = 22 * CHUNK
-AT_P2 = AT_HIDDEN_0
-AT_AA = AT_HIDDEN_0 + 2 * CHUNK
-AT_BB = AT_WEIGHTS_0
+AT_OUTPUT = {
+    "p2": (AT_HIDDEN_0, AT_GROUPED),
+    "aa": (AT_HIDDEN_0 + 2 * CHUNK, AT_GROUPED + CHUNK),
+    "bb": (AT_WEIGHTS_0, AT_GROUPED + 2 * CHUNK),
+    "wkv": (AT_PLANES, AT_GROUPED + 3 * CHUNK),
+}
 AT_P1 = AT_WEIGHTS_0 + 2 * CHUNK
 AT_QUOTIENT = 26 * CHUNK
 BY_DIFFERENCE = ((0, 0, 0), (0, 0, 1), (0, 1, 0), (0, 1, 1), (1, 0, 0), (1, 0, 1))
 E_CAP = 2.0**60
 AHEAD = 2
+G_PIECE = 128
 FIRST_SUMS = 4
+LATE = TILES - 2
 DOUBLE_SUMS = (1, 2, 3)
 SUM_AHEAD = 7
 
@@ -64,9 +69,16 @@ def interleave(nc, grouped, planes, shares):
         elif engine == "s":
             nc.scalar.copy(out=out, in_=in_)
         else:
-            nc.gpsimd.tensor_scalar(
-                out=out, in0=in_, scalar1=1.0, scalar2=0.0, op0=ALU.mult, op1=ALU.add
-            )
+            for piece in range(0, count // 4, G_PIECE // 4):
+                part = slice(piece, piece + G_PIECE // 4)
+                nc.gpsimd.tensor_scalar(
+                    out=out[:, part],
+                    in0=in_[:, part],
+                    scalar1=1.0,
+                    scalar2=0.0,
+                    op0=ALU.mult,
+                    op1=ALU.add,
+                )
 
 
 def quantise(nc, grouped, codes, scales):
@@ -146,17 +158,20 @@ def tile_rwkv_attention_pa_kernel(
                         stop=(sign is minus_ident),
                     )
 
-        def mix_turned_words(h, g, u, pool):
-            x_rows, s_rows = hidden_of[h, g]
+        def turn_saved(h, g, u, pool):
             s_turned = pool.tile([P, N_TILE], F32, name="s_turned")
-            turn_words(s_turned, s_rows, u)
-            first_diff = pool.tile([P, N_TILE], F32, name="x_turned")
-            turn_difference(first_diff, x_rows, s_rows, 2 * u)
+            turn_words(s_turned, hidden_of[h, g][1], u)
             s_words = arena.tile([P, N_TILE], F32, bufs=4, offset=AT_OLD, name="old_part")
             nc.scalar.copy(out=s_words[:], in_=s_turned[:])
-            second_diff = pool.tile([P, N_TILE], F32, name="s_turned")
-            turn_difference(second_diff, x_rows, s_rows, 2 * u + 1)
-            pair_of[h, g, u] = (s_words[:].bitcast(BF16), (first_diff, second_diff))
+            pair_of[h, g, u] = s_words[:].bitcast(BF16)
+
+        def turn_differences(h, g, u, pool):
+            diffs = []
+            for e, name in enumerate(("x_turned", "s_turned")):
+                diff = pool.tile([P, N_TILE], F32, name=name)
+                turn_difference(diff, *hidden_of[h, g], 2 * u + e)
+                diffs.append(diff)
+            pair_of[h, g, u] = (pair_of[h, g, u], diffs)
 
         def add_difference(h, g, u):
             old, diffs = pair_of[h, g, u]
@@ -240,7 +255,8 @@ def tile_rwkv_attention_pa_kernel(
 
         def turn(pool, h, g, u):
             if (h, g, u) in BY_DIFFERENCE:
-                mix_turned_words(h, g, u, pool)
+                turn_saved(h, g, u, pool)
+                turn_differences(h, g, u, pool)
                 return
             pair_of[h, g, u] = turn_pair(pool, g, u, *hidden_of[h, g])
 
@@ -320,8 +336,9 @@ def tile_rwkv_attention_pa_kernel(
             make_identity(nc, ident[:])
             make_identity(nc, ident_f32[:])
             nc.vector.tensor_scalar_mul(out=minus_ident[:], in0=ident[:], scalar1=-1.0)
-            mix_turned = turned.tile([P, PACK, P], BF16, tag="x_turned")
-            shift_turned = turned.tile([P, PACK, P], BF16, tag="s_turned")
+            turn_saved(0, 0, 0, turned)
+            mix_turned = early.tile([P, PACK, P], BF16, name="lead_turned")
+            shift_turned = early.tile([P, PACK, P], BF16, name="v_ps")
             for t in range(PACK):
                 nc.tensor.transpose(mix_turned[:, t, :], vector_rows[:, t:K_PASS:PACK], ident[:])
                 nc.tensor.transpose(
@@ -342,7 +359,7 @@ def tile_rwkv_attention_pa_kernel(
             nc.vector.tensor_tensor(out=shift[:], in0=decay, in1=first, op=ALU.add)
 
             V, S, G = (512, 0, 0), (0, 512, 0), (0, 0, 512)
-            turn(turned, 0, 0, 0)
+            turn_differences(0, 0, 0, turned)
             turn(turned_first, 0, 0, 1)
             for c, name in enumerate(("k_ps", "v_ps")):
                 spread = early.tile([P, N_TILE], F32, name=name)
@@ -371,10 +388,9 @@ def tile_rwkv_attention_pa_kernel(
             regroup("xv", 0, 1, V)
             pack("xk", 0, 1)
             pack("xv", 0, 0)
-            regroup("wv", 0, 1, S)
+            regroup("wv", 0, 1, V)
             pack("wk", 0, 1)
             pack("xv", 0, 1)
-            turn(turned, 1, 0, 0)
             pack("wv", 0, 1)
             regroup("wk", 1, 0, S)
 
@@ -475,10 +491,10 @@ def tile_rwkv_attention_pa_kernel(
                 out=out, in0=raw[:], scalar=cap, in1=other, op0=ALU.min, op1=op
             )
 
-        def quotient(i, e_ps, v_rows, num, den):
+        def quotient(i, e_ps, v_rows, num, den, adder):
             clamped(num, e_ps, v_rows[:], ALU.mult, E_CAP)
             clamped(den, e_ps, part_of(b_halves, i), ALU.add, E_CAP)
-            nc.gpsimd.tensor_tensor(out=num, in0=num, in1=part_of(a_halves, i), op=ALU.add)
+            adder.tensor_tensor(out=num, in0=num, in1=part_of(a_halves, i), op=ALU.add)
 
         def keep_state(i, f1_ps, bb):
             f1_a = work.tile([P, BLOCKS, P], F32)
@@ -494,13 +510,17 @@ def tile_rwkv_attention_pa_kernel(
 
         outputs = {}
 
-        def output_part(name, at, bufs, i):
+        def output_part(name, i):
             alone = i >= TILES - PAIR
+            at, at_alone = AT_OUTPUT[name]
             if alone or i % PAIR == 0:
-                tile = arena.tile(
-                    [P, BLOCKS, 1 if alone else PAIR, P], F32, name=name, bufs=bufs, offset=at
-                )
-                outputs[name] = tile
+                if alone:
+                    place = arena.tile(
+                        [P, BLOCKS, 1, P], F32, name=f"{name}_alone", bufs=2, offset=at_alone
+                    )
+                else:
+                    place = arena.tile([P, BLOCKS, PAIR, P], F32, name=name, bufs=2, offset=at)
+                outputs[name] = place
             return outputs[name][:, :, 0 if alone else i % PAIR, :]
 
         def store(out, name, i):
@@ -524,8 +544,8 @@ def tile_rwkv_attention_pa_kernel(
         }
         late_jobs = {
 
-            -2: [(regroup, "wv", 1, 0, V)],
-            -1: [(load_second_p,), (add, 1, 0, 0), (turn, turned, 1, 0, 1), (regroup, "wk", 1, 1, S), (regroup, "wv", 1, 1, S)],
+            -2: [(regroup, "wv", 1, 0, V), (turn, turned, 1, 0, 0)],
+            -1: [(load_second_p,), (add, 1, 0, 0), (turn, turned, 1, 0, 1), (regroup, "wk", 1, 1, S), (regroup, "wv", 1, 1, G)],
             0: [(add, 1, 0, 1), (turn, turned, 1, 1, 0), (regroup, "xk", 1, 0, S)],
             1: [(add, 1, 1, 0), (turn, turned, 1, 1, 1), (regroup, "xv", 1, 0, S)],
             2: [(load_second_state,), (add, 1, 1, 1), (regroup, "xk", 1, 1, S)],
@@ -552,7 +572,7 @@ def tile_rwkv_attention_pa_kernel(
         def finish(i, engine):
             num_done, den_done = num_den[i // GROUP]
             engine.tensor_tensor(
-                out=output_part("wkv", AT_PLANES, 4, i),
+                out=output_part("wkv", i),
                 in0=num_done[:, i % GROUP],
                 in1=den_done[:, i % GROUP],
                 op=ALU.mult,
@@ -562,7 +582,7 @@ def tile_rwkv_attention_pa_kernel(
         for s in range(-AHEAD, TILES):
             i = s + AHEAD
             if i < TILES:
-                raw[i] = compare(i, k_in[i], decayed_in[i], output_part("p2", AT_P2, 2, i))
+                raw[i] = compare(i, k_in[i], decayed_in[i], output_part("p2", i))
                 store(out_3, "p2", i)
             for job, *args in early_jobs.get(s, []):
                 job(*args)
@@ -588,9 +608,16 @@ def tile_rwkv_attention_pa_kernel(
                         [P, GROUP, BLOCKS, P], F32, name=f"den{odd}", offset=at + 2 * CHUNK
                     )
                     num_den[s // GROUP] = (num_group, den_group)
-                aa = output_part("aa", AT_AA, 2, s)
-                bb = output_part("bb", AT_BB, 2, s)
-                quotient(s, factor_in[s, 0], v_in[s], num_group[:, n], den_group[:, n])
+                aa = output_part("aa", s)
+                bb = output_part("bb", s)
+                quotient(
+                    s,
+                    factor_in[s, 0],
+                    v_in[s],
+                    num_group[:, n],
+                    den_group[:, n],
+                    nc.vector if s >= LATE else nc.gpsimd,
+                )
             if follows:
                 factor_in[s + 1, 0] = upright(raw[s + 1][0], "e_ps")
             if blends:

@@ -134,8 +134,7 @@ def tile_rwkv_attention_pa_kernel(
         mix = columns[:, 0 : 2 * CHUNKS]
         decay = columns[:, 2 * CHUNKS : 3 * CHUNKS]
         first = columns[:, 3 * CHUNKS : 4 * CHUNKS]
-        a0_rows = keep.tile([P, BLOCKS, WIDTH], BF16)
-        b0_rows = keep.tile([P, BLOCKS, WIDTH], BF16)
+        ab0_rows = keep.tile([P, 2, BLOCKS, WIDTH], BF16)
 
         def half_of(source, h):
             return source.rearrange("(h p r) d -> h p r d", r=BLOCKS, p=P)[h]
@@ -277,8 +276,14 @@ def tile_rwkv_attention_pa_kernel(
             add_pair(g, u, *pair_of[h, g, u], planes_of["xk", h, g], planes_of["xv", h, g])
 
         def regroup(name, h, g, shares):
+            early_chunk = h == 0 and g == 0
             grouped = arena.tile(
-                [P, N_TILE, PACK], BF16, bufs=4, align_bytes=64, offset=AT_GROUPED
+                [P, N_TILE, PACK],
+                BF16,
+                name="grouped_first" if early_chunk else "grouped",
+                bufs=4,
+                align_bytes=64,
+                offset=AT_QUOTIENT if early_chunk else AT_GROUPED,
             )
             interleave(nc, grouped[:], planes_of[name, h, g], shares)
             grouped_of[name, h, g] = grouped
@@ -322,16 +327,16 @@ def tile_rwkv_attention_pa_kernel(
                 p0_rows[c] = part
 
             load_first_hidden(0, between=load_vectors)
-            load_first_hidden(1)
             load_weights("wk", 0)
-            load_first_state(0)
+            load_first_hidden(1)
             load_weights("wv", 0)
+            load_first_state(0)
             load_weights("wk", 1)
             load_weights("wv", 1)
             load_second_hidden()
             load_first_state(1)
-            nc.sync.dma_start(out=a0_rows[:], in_=half_of(saved_a, 0))
-            nc.sync.dma_start(out=b0_rows[:], in_=half_of(saved_b, 0))
+            nc.sync.dma_start(out=ab0_rows[:, 0], in_=half_of(saved_a, 0))
+            nc.sync.dma_start(out=ab0_rows[:, 1], in_=half_of(saved_b, 0))
 
             make_identity(nc, ident[:])
             make_identity(nc, ident_f32[:])
@@ -361,6 +366,8 @@ def tile_rwkv_attention_pa_kernel(
             V, S, G = (512, 0, 0), (0, 512, 0), (0, 0, 512)
             turn_differences(0, 0, 0, turned)
             turn(turned_first, 0, 0, 1)
+            add(0, 0, 0)
+            turn(turned, 0, 1, 0)
             for c, name in enumerate(("k_ps", "v_ps")):
                 spread = early.tile([P, N_TILE], F32, name=name)
                 for j in range(BLOCKS):
@@ -370,24 +377,22 @@ def tile_rwkv_attention_pa_kernel(
                         ident_f32[:],
                     )
                 nc.scalar.copy(out=decay_rows[:, c * N_TILE : (c + 1) * N_TILE], in_=spread[:])
-            add(0, 0, 0)
-            turn(turned, 0, 1, 0)
             regroup("wk", 0, 0, G)
+            regroup("wv", 0, 0, G)
             add(0, 0, 1)
             turn(turned_first, 0, 1, 1)
-            regroup("wv", 0, 0, S)
-            add(0, 1, 0)
             regroup("xk", 0, 0, S)
+            add(0, 1, 0)
+            regroup("xv", 0, 0, S)
             add(0, 1, 1)
             pack("wk", 0, 0)
-            regroup("xv", 0, 0, S)
-            pack("wv", 0, 0)
+            regroup("wk", 0, 1, S)
             regroup("xk", 0, 1, V)
             pack("xk", 0, 0)
-            regroup("wk", 0, 1, S)
-            regroup("xv", 0, 1, V)
-            pack("xk", 0, 1)
             pack("xv", 0, 0)
+            regroup("xv", 0, 1, S)
+            pack("wv", 0, 0)
+            pack("xk", 0, 1)
             regroup("wv", 0, 1, V)
             pack("wk", 0, 1)
             pack("xv", 0, 1)
@@ -402,16 +407,13 @@ def tile_rwkv_attention_pa_kernel(
             nc.sync.dma_start(out=rows[:], in_=half_of(saved_p, 1))
             p1_rows.append(rows)
 
-        a_halves = [a0_rows]
-        b_halves = [b0_rows]
+        ab_halves = [ab0_rows]
 
         def load_second_state():
-            a1_rows = arena.tile([P, BLOCKS, WIDTH], BF16, offset=AT_HIDDEN_1)
-            b1_rows = arena.tile([P, BLOCKS, WIDTH], BF16, offset=AT_HIDDEN_1 + 2 * CHUNK)
-            nc.sync.dma_start(out=a1_rows[:], in_=half_of(saved_a, 1))
-            nc.sync.dma_start(out=b1_rows[:], in_=half_of(saved_b, 1))
-            a_halves.append(a1_rows)
-            b_halves.append(b1_rows)
+            ab1_rows = arena.tile([P, 2, BLOCKS, WIDTH], BF16, offset=AT_HIDDEN_1)
+            nc.sync.dma_start(out=ab1_rows[:, 0], in_=half_of(saved_a, 1))
+            nc.sync.dma_start(out=ab1_rows[:, 1], in_=half_of(saved_b, 1))
+            ab_halves.append(ab1_rows)
 
         def rows_of(i, b=0, count=BLOCKS):
             first_row = (i // COL_BLOCKS) * N_TILE + b * P
@@ -420,8 +422,8 @@ def tile_rwkv_attention_pa_kernel(
         def cols_of(i, count=1):
             return slice((i % COL_BLOCKS) * P, (i % COL_BLOCKS + count) * P)
 
-        def part_of(halves, i):
-            return halves[i // COL_BLOCKS][:, :, cols_of(i)]
+        def a_and_b(i):
+            return ab_halves[i // COL_BLOCKS][:, :, :, cols_of(i)]
 
         def project(i, acc, x_codes, x_scales, w_codes, w_scales):
             for b in range(BLOCKS):
@@ -442,7 +444,7 @@ def tile_rwkv_attention_pa_kernel(
             return k_ps
 
         def decay_state(i):
-            decayed = work.tile([P, BLOCKS, P], F32, bufs=SUM_AHEAD + 1)
+            decayed = work.tile([P, BLOCKS, P], F32, bufs=SUM_AHEAD)
             nc.gpsimd.tensor_tensor(
                 out=decayed[:],
                 in0=(
@@ -493,20 +495,26 @@ def tile_rwkv_attention_pa_kernel(
 
         def quotient(i, e_ps, v_rows, num, den, adder):
             clamped(num, e_ps, v_rows[:], ALU.mult, E_CAP)
-            clamped(den, e_ps, part_of(b_halves, i), ALU.add, E_CAP)
-            adder.tensor_tensor(out=num, in0=num, in1=part_of(a_halves, i), op=ALU.add)
+            clamped(den, e_ps, a_and_b(i)[:, 1], ALU.add, E_CAP)
+            adder.tensor_tensor(out=num, in0=num, in1=a_and_b(i)[:, 0], op=ALU.add)
 
-        def keep_state(i, f1_ps, bb):
-            f1_a = work.tile([P, BLOCKS, P], F32)
-            clamped(f1_a[:], f1_ps, part_of(a_halves, i), ALU.mult)
-            clamped(bb, f1_ps, part_of(b_halves, i), ALU.mult)
-            return f1_a
+        def keep_state(i, f1_ps):
+            kept = work.tile([P, 2, BLOCKS, P], F32)
+            nc.vector.scalar_tensor_tensor(
+                out=kept[:],
+                in0=f1_ps[:].unsqueeze(1).to_broadcast([P, 2, BLOCKS, P]),
+                scalar=1.0,
+                in1=a_and_b(i),
+                op0=ALU.min,
+                op1=ALU.mult,
+            )
+            return kept
 
-        def add_token(f2_ps, f1_a, v_rows, aa, bb, adder):
+        def add_token(f2_ps, kept, v_rows, aa, bb, adder):
             f2_v = work.tile([P, BLOCKS, P], F32)
             clamped(f2_v[:], f2_ps, v_rows[:], ALU.mult)
-            clamped(bb, f2_ps, bb, ALU.add)
-            adder.tensor_tensor(out=aa, in0=f1_a[:], in1=f2_v[:], op=ALU.add)
+            clamped(bb, f2_ps, kept[:, 1], ALU.add)
+            adder.tensor_tensor(out=aa, in0=kept[:, 0], in1=f2_v[:], op=ALU.add)
 
         outputs = {}
 
@@ -549,7 +557,7 @@ def tile_rwkv_attention_pa_kernel(
             0: [(add, 1, 0, 1), (turn, turned, 1, 1, 0), (regroup, "xk", 1, 0, S)],
             1: [(add, 1, 1, 0), (turn, turned, 1, 1, 1), (regroup, "xv", 1, 0, S)],
             2: [(load_second_state,), (add, 1, 1, 1), (regroup, "xk", 1, 1, S)],
-            3: [(regroup, "xv", 1, 1, S)],
+            3: [(regroup, "xv", 1, 1, G)],
         }
 
         k_in = {0: project_k(0)}
@@ -621,12 +629,12 @@ def tile_rwkv_attention_pa_kernel(
             if follows:
                 factor_in[s + 1, 0] = upright(raw[s + 1][0], "e_ps")
             if blends:
-                f1_a = keep_state(s, factor_in[s, 1], bb)
+                kept = keep_state(s, factor_in[s, 1])
             if follows:
                 factor_in[s + 1, 1] = upright(raw[s + 1][1], "f1_ps")
             if blends:
                 add_token(
-                    factor_in[s, 2], f1_a, v_in[s], aa, bb, nc.vector if s == TILES - 1 else nc.gpsimd
+                    factor_in[s, 2], kept, v_in[s], aa, bb, nc.vector if s == TILES - 1 else nc.gpsimd
                 )
                 store(out_2, "bb", s)
                 store(out_1, "aa", s)

from contextlib import ExitStack

import concourse.mybir as mybir
from concourse.masks import make_identity

F32 = mybir.dt.float32
BF16 = mybir.dt.bfloat16
U32 = mybir.dt.uint32
U8 = mybir.dt.uint8
FP8X4 = mybir.dt.float8_e4m3fn_x4
ALU = mybir.AluOpType
FUNC = mybir.ActivationFunctionType

P = 128
PACK = 4
K_PASS = P * PACK
ROWS = 1024
DEPTH = 1024
WIDTH = 1024
PASSES = DEPTH // K_PASS
CHUNKS = DEPTH // P
N_TILE = 512
ROW_HALVES = ROWS // N_TILE
COL_HALVES = WIDTH // N_TILE
BLOCKS = N_TILE // P
COL_BLOCKS = WIDTH // P
TILES = ROW_HALVES * COL_BLOCKS
GROUP = 4
PAIR = 2
CHUNK = PACK * N_TILE * 2
AT_HIDDEN_1 = 0
AT_WEIGHTS_1 = 4 * CHUNK
AT_PLANES = 8 * CHUNK
AT_GROUPED = 12 * CHUNK
AT_OLD = 16 * CHUNK
AT_HIDDEN_0 = 18 * CHUNK
AT_WEIGHTS_0 = 22 * CHUNK
AT_OUTPUT = {
    "p2": (AT_HIDDEN_0, AT_GROUPED),
    "aa": (AT_HIDDEN_0 + 2 * CHUNK, AT_GROUPED + CHUNK),
    "bb": (AT_WEIGHTS_0, AT_GROUPED + 2 * CHUNK),
    "wkv": (AT_PLANES, AT_GROUPED + 3 * CHUNK),
}
AT_P1 = AT_WEIGHTS_0 + 2 * CHUNK
AT_QUOTIENT = 26 * CHUNK
BY_DIFFERENCE = ((0, 0, 0), (0, 0, 1), (0, 1, 0), (0, 1, 1), (1, 0, 0), (1, 0, 1))
E_CAP = 2.0**60
AHEAD = 2
G_PIECE = 128
FIRST_SUMS = 4
LATE = TILES - 2
DOUBLE_SUMS = (1, 2, 3)
SUM_AHEAD = 7

FLOPS = 2 * 2 * ROWS * DEPTH * WIDTH


def interleave(nc, grouped, planes, shares):
    first = 0
    for engine, count in zip("vsg", shares):
        cols = slice(first, first + count)
        first += count
        if count == 0:
            continue
        out = grouped[:, cols, :].rearrange("p (c i) t -> p c t i", i=4)
        in_ = planes[:, :, cols].rearrange("p t (c i) -> p c t i", i=4)
        if engine == "v":
            nc.vector.tensor_copy(out=out, in_=in_)
        elif engine == "s":
            nc.scalar.copy(out=out, in_=in_)
        else:
            for piece in range(0, count // 4, G_PIECE // 4):
                part = slice(piece, piece + G_PIECE // 4)
                nc.gpsimd.tensor_scalar(
                    out=out[:, part],
                    in0=in_[:, part],
                    scalar1=1.0,
                    scalar2=0.0,
                    op0=ALU.mult,
                    op1=ALU.add,
                )


def quantise(nc, grouped, codes, scales):
    nc.vector.quantize_mx(
        out=codes.bitcast(FP8X4),
        scales=scales,
        in_=grouped.rearrange("p c t -> p (c t)"),
    )


def tile_rwkv_attention_pa_kernel(
    tc,
    x,
    saved_x,
    saved_a,
    saved_b,
    saved_p,
    time_decay,
    time_first,
    k_mixed,
    v_mixed,
    key_weight,
    value_weight,
    out_0,
    out_1,
    out_2,
    out_3,
):
    nc = tc.nc
    with ExitStack() as pools:
        pools.enter_context(tc.manual_schedule())
        keep = pools.enter_context(tc.tile_pool(name="keep", bufs=1))
        arena = pools.enter_context(tc.tile_pool(name="arena", bufs=1))
        work = pools.enter_context(tc.tile_pool(name="work", bufs=2))
        early = pools.enter_context(tc.psum_pool(name="early", bufs=1))

        xk_codes = keep.tile([P, PASSES, ROWS], U32, align_bytes=64)
        xv_codes = keep.tile([P, PASSES, ROWS], U32, align_bytes=64)
        wk_codes = keep.tile([P, PASSES, WIDTH], U32, align_bytes=64)
        wv_codes = keep.tile([P, PASSES, WIDTH], U32, align_bytes=64)
        xk_scales = keep.tile([P, PASSES, ROWS], U8, align_bytes=64)
        xv_scales = keep.tile([P, PASSES, ROWS], U8, align_bytes=64)
        wk_scales = keep.tile([P, PASSES, WIDTH], U8, align_bytes=64)
        wv_scales = keep.tile([P, PASSES, WIDTH], U8, align_bytes=64)
        decay_rows = keep.tile([P, WIDTH], BF16)
        ident = keep.tile([P, P], BF16)
        minus_ident = keep.tile([P, P], BF16)
        ident_f32 = keep.tile([P, P], F32)
        vector_rows = keep.tile([P, K_PASS], BF16)
        columns = keep.tile([P, 4 * CHUNKS], F32)
        one_minus_mix = keep.tile([P, 2 * CHUNKS], F32)
        shift = keep.tile([P, CHUNKS], F32)
        mix = columns[:, 0 : 2 * CHUNKS]
        decay = columns[:, 2 * CHUNKS : 3 * CHUNKS]
        first = columns[:, 3 * CHUNKS : 4 * CHUNKS]
        ab0_rows = keep.tile([P, 2, BLOCKS, WIDTH], BF16)

        def half_of(source, h):
            return source.rearrange("(h p r) d -> h p r d", r=BLOCKS, p=P)[h]

        def turn_words(bank, rows, u):
            words = rows.bitcast(F32)
            for b in range(BLOCKS):
                nc.tensor.transpose(
                    bank[:, b * P : (b + 1) * P], words[:, b, u : K_PASS // 2 : 2], ident_f32[:]
                )

        def turn_difference(bank, x_rows, s_rows, t):
            for b in range(BLOCKS):
                for rows, sign in ((x_rows, ident), (s_rows, minus_ident)):
                    nc.tensor.matmul(
                        bank[:, b * P : (b + 1) * P],
                        lhsT=rows[:, b, t:K_PASS:PACK],
                        rhs=sign[:],
                        start=(sign is ident),
                        stop=(sign is minus_ident),
                    )

        def turn_saved(h, g, u, pool):
            s_turned = pool.tile([P, N_TILE], F32, name="s_turned")
            turn_words(s_turned, hidden_of[h, g][1], u)
            s_words = arena.tile([P, N_TILE], F32, bufs=4, offset=AT_OLD, name="old_part")
            nc.scalar.copy(out=s_words[:], in_=s_turned[:])
            pair_of[h, g, u] = s_words[:].bitcast(BF16)

        def turn_differences(h, g, u, pool):
            diffs = []
            for e, name in enumerate(("x_turned", "s_turned")):
                diff = pool.tile([P, N_TILE], F32, name=name)
                turn_difference(diff, *hidden_of[h, g], 2 * u + e)
                diffs.append(diff)
            pair_of[h, g, u] = (pair_of[h, g, u], diffs)

        def add_difference(h, g, u):
            old, diffs = pair_of[h, g, u]
            for e in range(2):
                t = 2 * u + e
                c = g * PACK + t
                for name, col in (("xk", c), ("xv", CHUNKS + c)):
                    nc.vector.scalar_tensor_tensor(
                        out=planes_of[name, h, g][:, t, :],
                        in0=diffs[e][:],
                        scalar=mix[:, col : col + 1],
                        in1=old[:, e::2],
                        op0=ALU.mult,
                        op1=ALU.add,
                    )

        def turn_pair(pool, g, u, x_rows, s_rows):
            s_turned = pool.tile([P, N_TILE], F32, name="s_turned")
            x_turned = pool.tile([P, N_TILE], F32, name="x_turned")
            turn_words(s_turned, s_rows, u)
            turn_words(x_turned, x_rows, u)
            return s_turned, x_turned

        def scale_pair(g, u, s_turned):
            s_pairs = s_turned[:].bitcast(BF16)
            old_parts = []
            for e in range(2):
                c = g * PACK + 2 * u + e
                for col in (c, CHUNKS + c):
                    old_part = arena.tile([P, N_TILE], F32, bufs=4, offset=AT_OLD)
                    nc.scalar.activation(
                        out=old_part[:],
                        in_=s_pairs[:, e::2],
                        func=FUNC.Copy,
                        scale=one_minus_mix[:, col : col + 1],
                    )
                    old_parts.append(old_part)
            return old_parts

        def add_pair(g, u, x_turned, old_parts, k_planes, v_planes):
            x_pairs = x_turned[:].bitcast(BF16)
            for e in range(2):
                t = 2 * u + e
                c = g * PACK + t
                for n, (planes, col) in enumerate(((k_planes, c), (v_planes, CHUNKS + c))):
                    nc.vector.scalar_tensor_tensor(
                        out=planes[:, t, :],
                        in0=x_pairs[:, e::2],
                        scalar=mix[:, col : col + 1],
                        in1=old_parts[2 * e + n][:],
                        op0=ALU.mult,
                        op1=ALU.add,
                    )

        codes_of = {"xk": xk_codes, "xv": xv_codes, "wk": wk_codes, "wv": wv_codes}
        scales_of = {"xk": xk_scales, "xv": xv_scales, "wk": wk_scales, "wv": wv_scales}
        planes_of = {}
        grouped_of = {}
        pair_of = {}
        hidden_of = {}

        def load_first_hidden(g, between=None):
            depth = slice(g * K_PASS, (g + 1) * K_PASS)
            at = AT_HIDDEN_0 + 2 * g * CHUNK
            s_rows = arena.tile([P, BLOCKS, K_PASS], BF16, name=f"s0{g}", offset=at)
            x_rows = arena.tile([P, BLOCKS, K_PASS], BF16, name=f"x0{g}", offset=at + CHUNK)
            nc.sync.dma_start(out=s_rows[:], in_=half_of(saved_x, 0)[:, :, depth])
            if between is not None:
                between()
            nc.sync.dma_start(out=x_rows[:], in_=half_of(x, 0)[:, :, depth])
            hidden_of[0, g] = (x_rows[:], s_rows[:])

        def load_second_hidden():
            s_rows = arena.tile([P, BLOCKS, DEPTH], BF16, name="s1", offset=AT_HIDDEN_1)
            x_rows = arena.tile([P, BLOCKS, DEPTH], BF16, name="x1", offset=AT_HIDDEN_1 + 2 * CHUNK)
            nc.sync.dma_start(out=s_rows[:], in_=half_of(saved_x, 1))
            nc.sync.dma_start(out=x_rows[:], in_=half_of(x, 1))
            for g in range(PASSES):
                depth = slice(g * K_PASS, (g + 1) * K_PASS)
                hidden_of[1, g] = (x_rows[:, :, depth], s_rows[:, :, depth])

        def turn(pool, h, g, u):
            if (h, g, u) in BY_DIFFERENCE:
                turn_saved(h, g, u, pool)
                turn_differences(h, g, u, pool)
                return
            pair_of[h, g, u] = turn_pair(pool, g, u, *hidden_of[h, g])

        def scale(h, g, u):
            if (h, g, u) in BY_DIFFERENCE:
                return
            s_turned, x_turned = pair_of[h, g, u]
            pair_of[h, g, u] = (x_turned, scale_pair(g, u, s_turned))

        def add(h, g, u):
            if u == 0:
                for name in ("xk", "xv"):
                    planes = arena.tile([P, PACK, N_TILE], BF16, bufs=4, offset=AT_PLANES)
                    planes_of[name, h, g] = planes[:]
            if (h, g, u) in BY_DIFFERENCE:
                add_difference(h, g, u)
                return
            add_pair(g, u, *pair_of[h, g, u], planes_of["xk", h, g], planes_of["xv", h, g])

        def regroup(name, h, g, shares):
            early_chunk = h == 0 and g == 0
            grouped = arena.tile(
                [P, N_TILE, PACK],
                BF16,
                name="grouped_first" if early_chunk else "grouped",
                bufs=4,
                align_bytes=64,
                offset=AT_QUOTIENT if early_chunk else AT_GROUPED,
            )
            interleave(nc, grouped[:], planes_of[name, h, g], shares)
            grouped_of[name, h, g] = grouped

        def pack(name, h, g):
            part = slice(h * N_TILE, (h + 1) * N_TILE)
            quantise(
                nc, grouped_of[name, h, g][:], codes_of[name][:, g, part], scales_of[name][:, g, part]
            )

        turned = pools.enter_context(tc.psum_pool(name="turned", bufs=1))
        with ExitStack() as first_pools:
            turned_first = first_pools.enter_context(tc.psum_pool(name="turned_first", bufs=1))

            nc.vector.memset(vector_rows[:], 0.0)
            w_views = {
                "wk": key_weight.rearrange("(g p t) a -> g p t a", t=PACK, p=P),
                "wv": value_weight.rearrange("(g p t) a -> g p t a", t=PACK, p=P),
            }
            def load_weights(name, g):
                at = (AT_WEIGHTS_0, AT_WEIGHTS_1)[g] + (name == "wv") * 2 * CHUNK
                planes = arena.tile([P, PACK, WIDTH], BF16, name=f"{name}{g}", offset=at)
                nc.sync.dma_start(out=planes[:], in_=w_views[name][g])
                for c in range(COL_HALVES):
                    planes_of[name, c, g] = planes[:, :, c * N_TILE : (c + 1) * N_TILE]

            def load_vectors():
                for n, vector in enumerate((k_mixed, v_mixed, time_decay, time_first)):
                    nc.sync.dma_start(
                        out=vector_rows[n * PASSES : (n + 1) * PASSES, :],
                        in_=vector.rearrange("(g k) -> g k", k=K_PASS),
                    )

            p0_rows = {}

            def load_first_state(c):
                part = keep.tile([P, BLOCKS, N_TILE], BF16, name=f"p0{c}")
                nc.sync.dma_start(
                    out=part[:], in_=half_of(saved_p, 0)[:, :, c * N_TILE : (c + 1) * N_TILE]
                )
                p0_rows[c] = part

            load_first_hidden(0, between=load_vectors)
            load_weights("wk", 0)
            load_first_hidden(1)
            load_weights("wv", 0)
            load_first_state(0)
            load_weights("wk", 1)
            load_weights("wv", 1)
            load_second_hidden()
            load_first_state(1)
            nc.sync.dma_start(out=ab0_rows[:, 0], in_=half_of(saved_a, 0))
            nc.sync.dma_start(out=ab0_rows[:, 1], in_=half_of(saved_b, 0))

            make_identity(nc, ident[:])
            make_identity(nc, ident_f32[:])
            nc.vector.tensor_scalar_mul(out=minus_ident[:], in0=ident[:], scalar1=-1.0)
            turn_saved(0, 0, 0, turned)
            mix_turned = early.tile([P, PACK, P], BF16, name="lead_turned")
            shift_turned = early.tile([P, PACK, P], BF16, name="v_ps")
            for t in range(PACK):
                nc.tensor.transpose(mix_turned[:, t, :], vector_rows[:, t:K_PASS:PACK], ident[:])
                nc.tensor.transpose(
                    shift_turned[:, t, :], vector_rows[:, t * P : (t + 1) * P], ident[:]
                )
            for source, half in ((mix_turned, 0), (shift_turned, 1)):
                nc.vector.tensor_copy(
                    out=columns[:, half * 2 * CHUNKS : (half + 1) * 2 * CHUNKS].rearrange(
                        "p (r t) -> p r t", t=PACK
                    ),
                    in_=source[:, :, half * 2 * PASSES : (half + 1) * 2 * PASSES].rearrange(
                        "p t r -> p r t"
                    ),
                )
            nc.vector.tensor_scalar(
                out=one_minus_mix[:], in0=mix, scalar1=-1.0, scalar2=1.0, op0=ALU.mult, op1=ALU.add
            )
            nc.vector.tensor_tensor(out=shift[:], in0=decay, in1=first, op=ALU.add)

            V, S, G = (512, 0, 0), (0, 512, 0), (0, 0, 512)
            turn_differences(0, 0, 0, turned)
            turn(turned_first, 0, 0, 1)
            add(0, 0, 0)
            turn(turned, 0, 1, 0)
            for c, name in enumerate(("k_ps", "v_ps")):
                spread = early.tile([P, N_TILE], F32, name=name)
                for j in range(BLOCKS):
                    nc.tensor.transpose(
                        spread[:, j * P : (j + 1) * P],
                        decay[:, c * BLOCKS + j : c * BLOCKS + j + 1].to_broadcast([P, P]),
                        ident_f32[:],
                    )
                nc.scalar.copy(out=decay_rows[:, c * N_TILE : (c + 1) * N_TILE], in_=spread[:])
            regroup("wk", 0, 0, G)
            regroup("wv", 0, 0, G)
            add(0, 0, 1)
            turn(turned_first, 0, 1, 1)
            regroup("xk", 0, 0, S)
            add(0, 1, 0)
            regroup("xv", 0, 0, S)
            add(0, 1, 1)
            pack("wk", 0, 0)
            regroup("wk", 0, 1, S)
            regroup("xk", 0, 1, V)
            pack("xk", 0, 0)
            pack("xv", 0, 0)
            regroup("xv", 0, 1, S)
            pack("wv", 0, 0)
            pack("xk", 0, 1)
            regroup("wv", 0, 1, V)
            pack("wk", 0, 1)
            pack("xv", 0, 1)
            pack("wv", 0, 1)
            regroup("wk", 1, 0, S)

        banks = pools.enter_context(tc.psum_pool(name="banks", bufs=1, reuse_waits="tile"))
        p1_rows = []

        def load_second_p():
            rows = arena.tile([P, BLOCKS, WIDTH], BF16, name="p1_rows", offset=AT_P1)
            nc.sync.dma_start(out=rows[:], in_=half_of(saved_p, 1))
            p1_rows.append(rows)

        ab_halves = [ab0_rows]

        def load_second_state():
            ab1_rows = arena.tile([P, 2, BLOCKS, WIDTH], BF16, offset=AT_HIDDEN_1)
            nc.sync.dma_start(out=ab1_rows[:, 0], in_=half_of(saved_a, 1))
            nc.sync.dma_start(out=ab1_rows[:, 1], in_=half_of(saved_b, 1))
            ab_halves.append(ab1_rows)

        def rows_of(i, b=0, count=BLOCKS):
            first_row = (i // COL_BLOCKS) * N_TILE + b * P
            return slice(first_row, first_row + count * P)

        def cols_of(i, count=1):
            return slice((i % COL_BLOCKS) * P, (i % COL_BLOCKS + count) * P)

        def a_and_b(i):
            return ab_halves[i // COL_BLOCKS][:, :, :, cols_of(i)]

        def project(i, acc, x_codes, x_scales, w_codes, w_scales):
            for b in range(BLOCKS):
                for g in range(PASSES):
                    nc.tensor.matmul_mx(
                        out=acc[:, b, :],
                        lhsT=x_codes[:, g, rows_of(i, b, 1)].bitcast(FP8X4),
                        lhsT_scale=x_scales[:, g, rows_of(i, b, 1)],
                        rhs=w_codes[:, g, cols_of(i)].bitcast(FP8X4),
                        rhs_scale=w_scales[:, g, cols_of(i)],
                        start=(g == 0),
                        stop=(g == PASSES - 1),
                    )

        def project_k(i):
            k_ps = early.tile([P, BLOCKS, P], F32)
            project(i, k_ps, xk_codes, xk_scales, wk_codes, wk_scales)
            return k_ps

        def decay_state(i):
            decayed = work.tile([P, BLOCKS, P], F32, bufs=SUM_AHEAD)
            nc.gpsimd.tensor_tensor(
                out=decayed[:],
                in0=(
                    p1_rows[0][:, :, cols_of(i)]
                    if i >= COL_BLOCKS
                    else p0_rows[i * P // N_TILE][:, :, i * P % N_TILE : i * P % N_TILE + P]
                ),
                in1=decay_rows[:, cols_of(i)].unsqueeze(1).to_broadcast([P, BLOCKS, P]),
                op=ALU.add,
            )
            return decayed

        def project_v(i):
            v_ps = early.tile([P, BLOCKS, P], F32)
            project(i, v_ps, xv_codes, xv_scales, wv_codes, wv_scales)
            v_rows = work.tile([P, BLOCKS, P], F32, bufs=3)
            nc.scalar.copy(out=v_rows[:], in_=v_ps[:])
            return v_rows

        def compare(i, k_ps, decayed, p2):
            j = i % COL_BLOCKS
            lead = work.tile([P, BLOCKS, P], F32)
            nc.vector.tensor_tensor(out=lead[:], in0=k_ps[:], in1=decayed[:], op=ALU.subtract)
            nc.vector.tensor_tensor(out=p2, in0=k_ps[:], in1=decayed[:], op=ALU.max)
            lead_turned = early.tile([P, N_TILE], F32, name="lead_turned")
            for b in range(BLOCKS):
                nc.tensor.transpose(lead_turned[:, b * P : (b + 1) * P], lead[:, b, :], ident_f32[:])
            e_raw = work.tile([P, N_TILE], F32, bufs=AHEAD)
            f1_raw = work.tile([P, N_TILE], F32, bufs=AHEAD)
            f2_raw = work.tile([P, N_TILE], F32, bufs=AHEAD)
            nc.scalar.activation(
                out=e_raw[:], in_=lead_turned[:], func=FUNC.Exp, bias=shift[:, j : j + 1]
            )
            nc.scalar.activation(out=f1_raw[:], in_=lead_turned[:], func=FUNC.Exp, scale=-1.0)
            nc.scalar.activation(out=f2_raw[:], in_=lead_turned[:], func=FUNC.Exp)
            return e_raw, f1_raw, f2_raw

        def upright(turned_tile, name):
            bank = banks.tile([P, BLOCKS, P], F32, name=name)
            for b in range(BLOCKS):
                nc.tensor.transpose(bank[:, b, :], turned_tile[:, b * P : (b + 1) * P], ident_f32[:])
            return bank

        def clamped(out, raw, other, op, cap=1.0):
            nc.vector.scalar_tensor_tensor(
                out=out, in0=raw[:], scalar=cap, in1=other, op0=ALU.min, op1=op
            )

        def quotient(i, e_ps, v_rows, num, den, adder):
            clamped(num, e_ps, v_rows[:], ALU.mult, E_CAP)
            clamped(den, e_ps, a_and_b(i)[:, 1], ALU.add, E_CAP)
            adder.tensor_tensor(out=num, in0=num, in1=a_and_b(i)[:, 0], op=ALU.add)

        def keep_state(i, f1_ps):
            kept = work.tile([P, 2, BLOCKS, P], F32)
            nc.vector.scalar_tensor_tensor(
                out=kept[:],
                in0=f1_ps[:].unsqueeze(1).to_broadcast([P, 2, BLOCKS, P]),
                scalar=1.0,
                in1=a_and_b(i),
                op0=ALU.min,
                op1=ALU.mult,
            )
            return kept

        def add_token(f2_ps, kept, v_rows, aa, bb, adder):
            f2_v = work.tile([P, BLOCKS, P], F32)
            clamped(f2_v[:], f2_ps, v_rows[:], ALU.mult)
            clamped(bb, f2_ps, kept[:, 1], ALU.add)
            adder.tensor_tensor(out=aa, in0=kept[:, 0], in1=f2_v[:], op=ALU.add)

        outputs = {}

        def output_part(name, i):
            alone = i >= TILES - PAIR
            at, at_alone = AT_OUTPUT[name]
            if alone or i % PAIR == 0:
                if alone:
                    place = arena.tile(
                        [P, BLOCKS, 1, P], F32, name=f"{name}_alone", bufs=2, offset=at_alone
                    )
                else:
                    place = arena.tile([P, BLOCKS, PAIR, P], F32, name=name, bufs=2, offset=at)
                outputs[name] = place
            return outputs[name][:, :, 0 if alone else i % PAIR, :]

        def store(out, name, i):
            alone = i >= TILES - PAIR
            if alone or i % PAIR == PAIR - 1:
                count = 1 if alone else PAIR
                nc.sync.dma_start(
                    out=half_of(out, i // COL_BLOCKS)[:, :, cols_of(i - count + 1, count)],
                    in_=outputs[name][:].rearrange("p b n c -> p b (n c)"),
                )

        early_jobs = {

            -1: [(pack, "wk", 1, 0)],
            0: [(pack, "wv", 1, 0)],
            1: [(pack, "wk", 1, 1), (pack, "wv", 1, 1), (scale, 1, 1, 0)],
            2: [(pack, "xk", 1, 0), (scale, 1, 1, 1)],
            3: [(pack, "xv", 1, 0)],
            4: [(pack, "xk", 1, 1)],
            5: [(pack, "xv", 1, 1)],
        }
        late_jobs = {

            -2: [(regroup, "wv", 1, 0, V), (turn, turned, 1, 0, 0)],
            -1: [(load_second_p,), (add, 1, 0, 0), (turn, turned, 1, 0, 1), (regroup, "wk", 1, 1, S), (regroup, "wv", 1, 1, G)],
            0: [(add, 1, 0, 1), (turn, turned, 1, 1, 0), (regroup, "xk", 1, 0, S)],
            1: [(add, 1, 1, 0), (turn, turned, 1, 1, 1), (regroup, "xv", 1, 0, S)],
            2: [(load_second_state,), (add, 1, 1, 1), (regroup, "xk", 1, 1, S)],
            3: [(regroup, "xv", 1, 1, G)],
        }

        k_in = {0: project_k(0)}
        v_in = {}
        decayed_in = {i: decay_state(i) for i in range(FIRST_SUMS)}
        raw = {}
        factor_in = {}
        num_den = {}
        to_invert = []
        to_finish = []

        def logarithm(i, count=1):
            den_done = num_den[i // GROUP][1][:, i % GROUP : i % GROUP + count]
            nc.scalar.activation(out=den_done, in_=den_done, func=FUNC.Ln)

        def invert(i):
            den_done = num_den[i // GROUP][1][:, i % GROUP]
            nc.scalar.activation(out=den_done, in_=den_done, func=FUNC.Exp, scale=-1.0)

        def finish(i, engine):
            num_done, den_done = num_den[i // GROUP]
            engine.tensor_tensor(
                out=output_part("wkv", i),
                in0=num_done[:, i % GROUP],
                in1=den_done[:, i % GROUP],
                op=ALU.mult,
            )
            store(out_0, "wkv", i)

        for s in range(-AHEAD, TILES):
            i = s + AHEAD
            if i < TILES:
                raw[i] = compare(i, k_in[i], decayed_in[i], output_part("p2", i))
                store(out_3, "p2", i)
            for job, *args in early_jobs.get(s, []):
                job(*args)
            if i + 1 < TILES:
                k_in[i + 1] = project_k(i + 1)
            if 0 <= s + 2 < TILES:
                v_in[s + 2] = project_v(s + 2)
            for extra in range(2 if s in DOUBLE_SUMS else 1):
                if len(decayed_in) < TILES:
                    decayed_in[len(decayed_in)] = decay_state(len(decayed_in))
            for done in to_finish:
                finish(done, nc.gpsimd)
            to_finish = []
            blends = 0 <= s < TILES
            follows = 0 <= s + 1 < TILES
            if blends:
                n = s % GROUP
                if n == 0:
                    odd = (s // GROUP) % 2
                    at = (AT_QUOTIENT, AT_WEIGHTS_1)[odd]
                    num_group = arena.tile([P, GROUP, BLOCKS, P], F32, name=f"num{odd}", offset=at)
                    den_group = arena.tile(
                        [P, GROUP, BLOCKS, P], F32, name=f"den{odd}", offset=at + 2 * CHUNK
                    )
                    num_den[s // GROUP] = (num_group, den_group)
                aa = output_part("aa", s)
                bb = output_part("bb", s)
                quotient(
                    s,
                    factor_in[s, 0],
                    v_in[s],
                    num_group[:, n],
                    den_group[:, n],
                    nc.vector if s >= LATE else nc.gpsimd,
                )
            if follows:
                factor_in[s + 1, 0] = upright(raw[s + 1][0], "e_ps")
            if blends:
                kept = keep_state(s, factor_in[s, 1])
            if follows:
                factor_in[s + 1, 1] = upright(raw[s + 1][1], "f1_ps")
            if blends:
                add_token(
                    factor_in[s, 2], kept, v_in[s], aa, bb, nc.vector if s == TILES - 1 else nc.gpsimd
                )
                store(out_2, "bb", s)
                store(out_1, "aa", s)
            if follows:
                factor_in[s + 1, 2] = upright(raw[s + 1][2], "f2_ps")
            if s >= 0 and s % GROUP == GROUP - 1 and s < TILES - 1:
                to_invert += range(s - GROUP + 1, s + 1)
                logarithm(s - GROUP + 1, GROUP)
            if to_invert:
                invert(to_invert[0])
                to_finish.append(to_invert.pop(0))
            if s == TILES - AHEAD:
                for done in range(TILES - GROUP, s):
                    logarithm(done)
            if s >= TILES - AHEAD:
                logarithm(s)
            for job, *args in late_jobs.get(s, []):
                job(*args)
        for done in to_finish:
            finish(done, nc.gpsimd)
        for done in range(TILES - GROUP, TILES):
            invert(done)
            finish(done, nc.vector)
